import numpy as np
import ml_dtypes


def mxq(x, axis, fmt="e4m3"):
    dtype, down = {"e4m3": (ml_dtypes.float8_e4m3fn, 7), "e5m2": (ml_dtypes.float8_e5m2, 14)}[fmt]
    v = np.moveaxis(np.asarray(x, np.float32).astype(ml_dtypes.bfloat16).astype(np.float64), axis, -1)
    blocks = v.reshape(v.shape[:-1] + (-1, 32))
    amax = np.abs(blocks).max(-1, keepdims=True)
    byte = np.maximum(np.where(amax > 0, np.frexp(amax)[1] - 1 + 127, 0) - down, 1)
    scale = np.exp2(byte - 127.0)
    codes = (blocks / scale).astype(np.float32).astype(dtype).astype(np.float64)
    return np.moveaxis((codes * scale).reshape(v.shape), -1, axis)


WIDE = False


def mx_kscale(k):
    if not WIDE:
        return np.ones(k)
    levels = np.array([10, -10, 5, -5, 0])
    a = np.random.permutation(np.resize(levels, k // 512 * 4)).reshape(k // 512, 4)
    idx = np.arange(k)
    return np.exp2(a[idx // 512, idx % 128 // 32])


BF16 = ml_dtypes.bfloat16


def bf(x):
    return np.asarray(x, np.float32).astype(BF16)


def f64(x):
    return np.asarray(x).astype(np.float64)


E2M1 = np.array([0.0, 0.5, 1.0, 1.5, 2.0, 3.0, 4.0, 6.0, -0.0, -0.5, -1.0, -1.5, -2.0, -3.0, -4.0, -6.0])


def pack_weight(w, fmt):
    k, n = w.shape
    w = f64(bf(w)).reshape(k // 32, 32, n)
    amax = np.abs(w).max(1)
    if fmt == "e4m3":
        byte = np.frexp(amax)[1] - 1 + 127 - 7
    else:
        mant, ex = np.frexp(amax / 6.0)
        byte = np.where(mant > 0.5, ex, ex - 1) + 127
    byte = np.clip(np.where(amax > 0, byte, 1), 1, 254)
    scaled = (w * np.exp2(127.0 - byte)[:, None, :]).reshape(k, n).astype(np.float32)
    by_word = np.ascontiguousarray(scaled.reshape(k // 512, 128, 4, n).transpose(0, 1, 3, 2))
    if fmt == "e4m3":
        words = by_word.astype(ml_dtypes.float8_e4m3fn).view(np.uint8)
    else:
        c = by_word.astype(ml_dtypes.float4_e2m1fn).view(np.uint8) & 0xF
        words = c[..., 0::2] | (c[..., 1::2] << 4)
    return np.ascontiguousarray(words), np.ascontiguousarray(byte.astype(np.uint8).reshape(k // 512, 16, n))


def unpack_weight(words, scales, fmt):
    g, p, n, _ = words.shape
    if fmt == "e4m3":
        vals = np.ascontiguousarray(words).view(ml_dtypes.float8_e4m3fn).astype(np.float64)
    else:
        nib = np.empty((g, p, n, 4), np.uint8)
        nib[..., 0::2] = words & 0xF
        nib[..., 1::2] = words >> 4
        vals = E2M1[nib]
    vals = vals * np.repeat(np.exp2(scales.astype(np.float64) - 127.0), 8, axis=1)[..., None]
    return vals.transpose(0, 1, 3, 2).reshape(g * 512, n)

def pack4(w):
    words, scales = pack_weight(w, "e2m1")
    return words.reshape(words.shape[0], 128, -1), scales


def unpack4(words, scales):
    return unpack_weight(words.reshape(words.shape[0], 128, -1, 2), scales, "e2m1")


N, F, E, H, R = 512, 512, 512, 4, 8
EPS = 1e-6


def setup_inputs():
    s = mx_kscale(F)
    c = 4.0 / np.sqrt(E)
    B = np.random.standard_normal((R, E)) / np.sqrt(R)
    W = c * (0.8 * np.random.standard_normal((F, R)) @ B + 0.6 * np.random.standard_normal((F, E))) / np.sqrt(F)
    Z = c * (0.8 * np.random.standard_normal((H, N, R)) @ B + 0.6 * np.random.standard_normal((H, N, E)))
    W_words, W_scales = pack4(W / s[:, None])
    return {"X": bf(np.random.standard_normal((N, F)) * s), "W_words": W_words, "W_scales": W_scales, "Z": bf(Z),
            "beta": bf(1.5 + 0.5 * np.random.random(1))}


def reference(X, W_words, W_scales, Z, beta):
    Zf = f64(Z)
    X_emb = mxq(f64(X), 1, "e4m3") @ unpack4(W_words, W_scales)
    aff = mxq(Zf, 2, "e4m3") @ mxq(X_emb, 1, "e4m3").T
    X_norm = np.sqrt(np.sum(X_emb * X_emb, axis=-1))
    Z_norm = np.sqrt(np.sum(Zf * Zf, axis=-1))
    aff = aff / (X_norm[None, None, :] + EPS)
    aff = aff / (Z_norm[:, :, None] + EPS)
    aff = np.max(aff, axis=0)
    aff = (aff + aff.T) / 2.0
    aff = (aff + 1.0) / 2.0
    return np.power(aff, f64(beta))

@@ -1,0 +1,308 @@
+from contextlib import ExitStack
+
+import concourse.mybir as mybir
+from concourse.masks import make_identity
+
+F32 = mybir.dt.float32
+BF16 = mybir.dt.bfloat16
+I32 = mybir.dt.int32
+U32 = mybir.dt.uint32
+U8 = mybir.dt.uint8
+FP8X4 = mybir.dt.float8_e4m3fn_x4
+FP4X4 = mybir.dt.float4_e2m1fn_x4
+ACT = mybir.ActivationFunctionType
+ALU = mybir.AluOpType
+
+P = 128
+PACK = 4
+NODES = 512
+FEATURES = 512
+EMBED = 512
+HEADS = 4
+TILES = NODES // P
+EPS = 1e-6
+
+FLOPS = 2 * NODES * FEATURES * EMBED + 2 * HEADS * NODES * NODES * EMBED
+
+
+def tile_affnet_kernel(tc, X, W_words, W_scales, Z, beta, out):
+    nc = tc.nc
+    with ExitStack() as ctx:
+        keep = ctx.enter_context(tc.tile_pool(name="keep", bufs=1))
+        work = ctx.enter_context(tc.tile_pool(name="work", bufs=2))
+        psum_t = ctx.enter_context(tc.psum_pool(name="psum_t", bufs=4))
+        psum_m = ctx.enter_context(tc.psum_pool(name="psum_m", bufs=4))
+        ctx.enter_context(tc.manual_schedule())
+
+        w_plane = keep.tile([P, EMBED], U8, align_bytes=64)
+        nc.vector.memset(w_plane[:].bitcast(I32), 0)
+        half = keep.tile([P, 1], F32)
+        nc.vector.memset(half[:], 0.5)
+        root = keep.tile([P, HEADS], F32)
+        nc.vector.memset(root[:], 0.5)
+        warm = keep.tile([P, 1], F32)
+        nc.scalar.activation(out=warm[:], in_=half[:], func=ACT.Ln)
+        ident_f = keep.tile([P, P], F32)
+        make_identity(nc, ident_f[:])
+        ident_b = keep.tile([P, P], BF16)
+        make_identity(nc, ident_b[:])
+
+        x_sb = keep.tile([P, TILES, FEATURES], BF16)
+        x_rows = X.rearrange("(a p) f -> p a f", p=P)
+        for b in range(2):
+            nc.sync.dma_start(out=x_sb[:, 2 * b : 2 * b + 2, :], in_=x_rows[:, 2 * b : 2 * b + 2, :])
+        for q in range(4):
+            nc.sync.dma_start(
+                out=w_plane[32 * q : 32 * q + 4, :].bitcast(I32),
+                in_=W_scales[0, 4 * q : 4 * q + 4, :].bitcast(I32),
+            )
+        w_words = keep.tile([P, 2 * EMBED], U8, align_bytes=64)
+        nc.sync.dma_start(out=w_words[:].bitcast(I32), in_=W_words[0].bitcast(I32))
+        z_sb = keep.tile([P, TILES, HEADS, EMBED], BF16)
+        for j in range(TILES):
+            nc.sync.dma_start(
+                out=z_sb[:, j], in_=Z[:, j * P : (j + 1) * P, :].rearrange("h p e -> p h e")
+            )
+        beta_b = keep.tile([P, 1], BF16)
+        nc.sync.dma_start(out=beta_b[:], in_=beta.partition_broadcast(P))
+
+        x_grouped = keep.tile([P, TILES, P, PACK], BF16, align_bytes=64)
+        x_codes = keep.tile([P, NODES], U32, align_bytes=64)
+        x_scales = keep.tile([P, NODES], U8, align_bytes=64)
+        xe_bf = keep.tile([P, TILES, PACK, P], BF16)
+        xe_grouped = keep.tile([P, TILES, P, PACK], BF16, align_bytes=64)
+        xe_codes = keep.tile([P, NODES], U32, align_bytes=64)
+        xe_scales = keep.tile([P, NODES], U8, align_bytes=64)
+        x_sumsq = keep.tile([P, TILES], F32)
+        x_root = keep.tile([P, TILES], F32)
+        x_norm = keep.tile([P, TILES], F32)
+        x_inv = keep.tile([P, TILES], F32)
+        x_inv_row = keep.tile([P, NODES], F32)
+        z_grouped = keep.tile([P, TILES, HEADS, P, PACK], BF16, align_bytes=64)
+        z_codes = keep.tile([P, TILES, HEADS * P], U32, align_bytes=64)
+        z_scales = keep.tile([P, TILES, HEADS * P], U8, align_bytes=64)
+        z_sumsq = keep.tile([P, TILES, HEADS], F32)
+        z_root = keep.tile([P, TILES, HEADS], F32)
+        z_norm = keep.tile([P, TILES, HEADS], F32)
+        z_inv = keep.tile([P, TILES, HEADS], F32)
+        best = keep.tile([P, TILES, NODES], F32)
+        logs = keep.tile([P, TILES, NODES], F32)
+        result = keep.tile([P, TILES, NODES], F32)
+        beta_f = keep.tile([P, 1], F32)
+
+        def transpose_x(b):
+            x_t = psum_t.tile([P, 2, 2, P], F32, tag="t")
+            for a in range(2):
+                for u in range(2):
+                    nc.tensor.transpose(
+                        x_t[:, a, u, :],
+                        x_sb[:, 2 * b + a, :].bitcast(F32)[:, u : FEATURES // 2 : 2],
+                        ident_f[:],
+                    )
+            return x_t
+
+        def quantise_half(grouped, codes, scales, b):
+            cols = slice(2 * b * P, (2 * b + 2) * P)
+            nc.vector.quantize_mx(
+                out=codes[:, cols].bitcast(FP8X4),
+                scales=scales[:, cols],
+                in_=grouped[:, 2 * b : 2 * b + 2].rearrange("p a m t -> p (a m t)"),
+            )
+
+        def embed(a):
+            xe_ps = psum_m.tile([P, EMBED], F32, tag="m")
+            nc.tensor.matmul_mx(
+                out=xe_ps[:],
+                lhsT=x_codes[:, a * P : (a + 1) * P].bitcast(FP8X4),
+                lhsT_scale=x_scales[:, a * P : (a + 1) * P],
+                rhs=w_words[:].bitcast(FP4X4),
+                rhs_scale=w_plane[:],
+                start=True,
+                stop=True,
+            )
+            return xe_ps
+
+        def transpose_xe(b):
+            xe_t = psum_t.tile([P, 2, PACK, P], BF16, tag="t")
+            for a in range(2):
+                for t in range(PACK):
+                    nc.tensor.transpose(xe_t[:, a, t, :], xe_bf[:, 2 * b + a, t, :], ident_b[:])
+            return xe_t
+
+        def transpose_z(j):
+            banks = []
+            for hb in range(2):
+                z_t = psum_t.tile([P, 2, 2, P], F32, tag="t")
+                for h in range(2):
+                    for u in range(2):
+                        nc.tensor.transpose(
+                            z_t[:, h, u, :],
+                            z_sb[:, j, 2 * hb + h, :].bitcast(F32)[:, u * P : (u + 1) * P],
+                            ident_f[:],
+                        )
+                banks.append(z_t)
+            return banks
+
+        def move_z(j, hb, z_t):
+            nc.vector.tensor_copy(
+                out=z_grouped[:, j, 2 * hb : 2 * hb + 2].bitcast(F32),
+                in_=z_t[:].rearrange("p h u n -> p h n u"),
+            )
+
+        def square_z(j, h):
+            squares = work.tile([P, EMBED], BF16)
+            nc.scalar.activation(
+                out=squares[:], in_=z_sb[:, j, h, :], func=ACT.Square,
+                accum_out=z_sumsq[:, j, h : h + 1],
+            )
+
+        def quantise_z(j):
+            nc.vector.quantize_mx(
+                out=z_codes[:, j, :].bitcast(FP8X4),
+                scales=z_scales[:, j, :],
+                in_=z_grouped[:, j].rearrange("p h n t -> p (h n t)"),
+            )
+
+        def multiply(j):
+            banks = []
+            for h in range(HEADS):
+                aff_ps = psum_m.tile([P, NODES], F32, tag="m")
+                nc.tensor.matmul_mx(
+                    out=aff_ps[:],
+                    lhsT=z_codes[:, j, h * P : (h + 1) * P].bitcast(FP8X4),
+                    lhsT_scale=z_scales[:, j, h * P : (h + 1) * P],
+                    rhs=xe_codes[:].bitcast(FP8X4),
+                    rhs_scale=xe_scales[:],
+                    start=True,
+                    stop=True,
+                )
+                banks.append(aff_ps)
+            return banks
+
+        def flip(j):
+            width = (j + 1) * P
+            flipped = psum_t.tile([P, NODES], F32, tag="t")
+            for i in range(j + 1):
+                nc.tensor.transpose(
+                    flipped[:, i * P : (i + 1) * P], best[:, i, j * P : (j + 1) * P], ident_f[:]
+                )
+            direct = work.tile([P, NODES], F32)
+            nc.gpsimd.tensor_tensor(
+                out=direct[:, :width], in0=best[:, j, :width], in1=x_inv_row[:, :width], op=ALU.mult
+            )
+            return flipped, direct
+
+        def symmetrise(j, flipped, direct):
+            width = (j + 1) * P
+            both = work.tile([P, NODES], F32)
+            nc.vector.scalar_tensor_tensor(
+                out=both[:, :width], in0=flipped[:, :width], scalar=x_inv[:, j : j + 1],
+                in1=direct[:, :width], op0=ALU.mult, op1=ALU.add,
+            )
+            nc.scalar.activation(
+                out=logs[:, j, :width], in_=both[:, :width], func=ACT.Ln, scale=0.25, bias=half[:]
+            )
+
+        x_t0 = transpose_x(0)
+        x_t1 = transpose_x(1)
+        nc.vector.tensor_copy(out=x_grouped[:, 0:2].bitcast(F32), in_=x_t0[:].rearrange("p a u m -> p a m u"))
+        nc.scalar.copy(out=x_grouped[:, 2:4].bitcast(F32), in_=x_t1[:].rearrange("p a u m -> p a m u"))
+        quantise_half(x_grouped, x_codes, x_scales, 0)
+        quantise_half(x_grouped, x_codes, x_scales, 1)
+        z_banks = transpose_z(0)
+        xe_banks = [embed(a) for a in range(TILES)]
+        square_z(0, 0)
+        square_z(0, 1)
+        move_z(0, 0, z_banks[0])
+        for a in range(TILES):
+            copy = nc.vector.tensor_copy if a % 2 == 0 else nc.scalar.copy
+            copy(
+                out=xe_bf[:, a].rearrange("p (u c) q -> p u c q", u=2),
+                in_=xe_banks[a][:].rearrange("p (u q c) -> p u c q", u=2, c=2),
+            )
+        xe_t0 = transpose_xe(0)
+        move_z(0, 1, z_banks[1])
+        square_z(0, 2)
+        xe_t1 = transpose_xe(1)
+        nc.vector.tensor_copy(out=xe_grouped[:, 0:2], in_=xe_t0[:].rearrange("p a t m -> p a m t"))
+        nc.scalar.copy(out=xe_grouped[:, 2:4], in_=xe_t1[:].rearrange("p a t m -> p a m t"))
+        xe_banks = [embed(a) for a in range(TILES)]
+        z_banks = transpose_z(1)
+        quantise_z(0)
+        quantise_half(xe_grouped, xe_codes, xe_scales, 0)
+        quantise_half(xe_grouped, xe_codes, xe_scales, 1)
+        square_z(0, 3)
+        nc.gpsimd.tensor_tensor(out=z_root[:, 0], in0=z_sumsq[:, 0], in1=root[:], op=ALU.pow)
+        for a in range(TILES):
+            squares_x = work.tile([P, EMBED], BF16)
+            nc.scalar.activation(
+                out=squares_x[:], in_=xe_banks[a][:], func=ACT.Square, accum_out=x_sumsq[:, a : a + 1]
+            )
+        nc.gpsimd.tensor_tensor(out=x_root[:], in0=x_sumsq[:], in1=root[:], op=ALU.pow)
+        nc.vector.tensor_scalar_add(out=z_norm[:, 0], in0=z_root[:, 0], scalar1=EPS)
+        nc.vector.reciprocal(out=z_inv[:, 0], in_=z_norm[:, 0])
+        aff_banks = multiply(0)
+
+        pending = None
+        for j in range(TILES):
+            first = work.tile([P, NODES], F32, name="running", bufs=4)
+            nc.scalar.activation(out=first[:], in_=aff_banks[0][:], func=ACT.Copy, scale=z_inv[:, j, 0:1])
+            if j + 1 < TILES:
+                move_z(j + 1, 0, z_banks[0])
+                move_z(j + 1, 1, z_banks[1])
+                for h in range(HEADS):
+                    square_z(j + 1, h)
+                nc.gpsimd.tensor_tensor(
+                    out=z_root[:, j + 1], in0=z_sumsq[:, j + 1], in1=root[:], op=ALU.pow
+                )
+            if j + 2 < TILES:
+                z_banks = transpose_z(j + 2)
+            if pending is not None:
+                symmetrise(j - 1, pending[0], pending[1])
+            if j + 1 < TILES:
+                quantise_z(j + 1)
+            running = first[:]
+            for h in range(1, HEADS):
+                if h == HEADS - 1:
+                    larger = best[:, j, :]
+                else:
+                    larger = work.tile([P, NODES], F32, name="running", bufs=4)[:]
+                nc.vector.scalar_tensor_tensor(
+                    out=larger, in0=aff_banks[h][:], scalar=z_inv[:, j, h : h + 1], in1=running,
+                    op0=ALU.mult, op1=ALU.max,
+                )
+                running = larger
+            if j + 1 < TILES:
+                aff_banks = multiply(j + 1)
+                nc.vector.tensor_scalar_add(out=z_norm[:, j + 1], in0=z_root[:, j + 1], scalar1=EPS)
+                nc.vector.reciprocal(out=z_inv[:, j + 1], in_=z_norm[:, j + 1])
+            if j == 0:
+                nc.vector.tensor_scalar_add(out=x_norm[:], in0=x_root[:], scalar1=EPS)
+                nc.vector.reciprocal(out=x_inv[:], in_=x_norm[:])
+                nc.vector.tensor_copy(out=beta_f[:], in_=beta_b[:])
+                row_ps = psum_t.tile([P, NODES], F32, tag="t")
+                for a in range(TILES):
+                    nc.tensor.matmul(
+                        out=row_ps[:, a * P : (a + 1) * P],
+                        lhsT=x_inv[:, a : a + 1].to_broadcast([P, P]),
+                        rhs=ident_f[:],
+                        start=True,
+                        stop=True,
+                    )
+                nc.scalar.copy(out=x_inv_row[:], in_=row_ps[:])
+            pending = flip(j)
+        symmetrise(TILES - 1, pending[0], pending[1])
+
+        mirrors = [psum_t.tile([P, NODES], F32, name="mirror%d" % i, tag="t") for i in range(TILES - 1)]
+        for j in reversed(range(TILES)):
+            width = (j + 1) * P
+            nc.scalar.activation(
+                out=result[:, j, :width], in_=logs[:, j, :width], func=ACT.Exp, scale=beta_f[:]
+            )
+            for i in range(j):
+                nc.tensor.transpose(
+                    mirrors[i][:, j * P : (j + 1) * P], result[:, j, i * P : (i + 1) * P], ident_f[:]
+                )
+            if width < NODES:
+                nc.vector.tensor_copy(out=result[:, j, width:], in_=mirrors[j][:, width:])
+            nc.sync.dma_start(out=out[j * P : (j + 1) * P, :], in_=result[:, j, :])

@@ -47,7 +47,19 @@ def tile_affnet_kernel(tc, X, W_words, W_scales, Z, beta, out):
         ident_b = keep.tile([P, P], BF16)
         make_identity(nc, ident_b[:])
 
+        z_sb = keep.tile([P, TILES, HEADS, EMBED], BF16)
         x_sb = keep.tile([P, TILES, FEATURES], BF16)
+        w_words = keep.tile([P, 2 * EMBED], U8, align_bytes=64)
+        beta_b = keep.tile([P, 1], BF16)
+
+        def load_z(j):
+            for hb in range(2):
+                nc.sync.dma_start(
+                    out=z_sb[:, j, 2 * hb : 2 * hb + 2, :],
+                    in_=Z[2 * hb : 2 * hb + 2, j * P : (j + 1) * P, :].rearrange("h p e -> p h e"),
+                )
+
+        load_z(0)
         x_rows = X.rearrange("(a p) f -> p a f", p=P)
         for b in range(2):
             nc.sync.dma_start(out=x_sb[:, 2 * b : 2 * b + 2, :], in_=x_rows[:, 2 * b : 2 * b + 2, :])
@@ -56,14 +68,9 @@ def tile_affnet_kernel(tc, X, W_words, W_scales, Z, beta, out):
                 out=w_plane[32 * q : 32 * q + 4, :].bitcast(I32),
                 in_=W_scales[0, 4 * q : 4 * q + 4, :].bitcast(I32),
             )
-        w_words = keep.tile([P, 2 * EMBED], U8, align_bytes=64)
         nc.sync.dma_start(out=w_words[:].bitcast(I32), in_=W_words[0].bitcast(I32))
-        z_sb = keep.tile([P, TILES, HEADS, EMBED], BF16)
-        for j in range(TILES):
-            nc.sync.dma_start(
-                out=z_sb[:, j], in_=Z[:, j * P : (j + 1) * P, :].rearrange("h p e -> p h e")
-            )
-        beta_b = keep.tile([P, 1], BF16)
+        for j in range(1, TILES):
+            load_z(j)
         nc.sync.dma_start(out=beta_b[:], in_=beta.partition_broadcast(P))
 
         x_grouped = keep.tile([P, TILES, P, PACK], BF16, align_bytes=64)
@@ -86,6 +93,8 @@ def tile_affnet_kernel(tc, X, W_words, W_scales, Z, beta, out):
         z_norm = keep.tile([P, TILES, HEADS], F32)
         z_inv = keep.tile([P, TILES, HEADS], F32)
         best = keep.tile([P, TILES, NODES], F32)
+        direct = keep.tile([P, TILES, NODES], F32)
+        both = keep.tile([P, TILES, NODES], F32)
         logs = keep.tile([P, TILES, NODES], F32)
         result = keep.tile([P, TILES, NODES], F32)
         beta_f = keep.tile([P, 1], F32)
@@ -179,41 +188,55 @@ def tile_affnet_kernel(tc, X, W_words, W_scales, Z, beta, out):
                 banks.append(aff_ps)
             return banks
 
+        def invert_z_norm(j):
+            nc.vector.tensor_scalar_add(out=z_norm[:, j], in0=z_root[:, j], scalar1=EPS)
+            nc.vector.reciprocal(out=z_inv[:, j], in_=z_norm[:, j])
+
+        def root_z(j):
+            nc.gpsimd.tensor_tensor(out=z_root[:, j], in0=z_sumsq[:, j], in1=root[:], op=ALU.pow)
+
         def flip(j):
-            width = (j + 1) * P
             flipped = psum_t.tile([P, NODES], F32, tag="t")
             for i in range(j + 1):
                 nc.tensor.transpose(
                     flipped[:, i * P : (i + 1) * P], best[:, i, j * P : (j + 1) * P], ident_f[:]
                 )
-            direct = work.tile([P, NODES], F32)
-            nc.gpsimd.tensor_tensor(
-                out=direct[:, :width], in0=best[:, j, :width], in1=x_inv_row[:, :width], op=ALU.mult
-            )
-            return flipped, direct
+            return flipped
 
-        def symmetrise(j, flipped, direct):
+        def scale_columns(j):
             width = (j + 1) * P
-            both = work.tile([P, NODES], F32)
+            nc.gpsimd.tensor_tensor(
+                out=direct[:, j, :width], in0=best[:, j, :width], in1=x_inv_row[:, :width], op=ALU.mult
+            )
+
+        def symmetrise(j, flipped):
+            width = (j + 1) * P
             nc.vector.scalar_tensor_tensor(
-                out=both[:, :width], in0=flipped[:, :width], scalar=x_inv[:, j : j + 1],
-                in1=direct[:, :width], op0=ALU.mult, op1=ALU.add,
+                out=both[:, j, :width], in0=flipped[:, :width], scalar=x_inv[:, j : j + 1],
+                in1=direct[:, j, :width], op0=ALU.mult, op1=ALU.add,
             )
             nc.scalar.activation(
-                out=logs[:, j, :width], in_=both[:, :width], func=ACT.Ln, scale=0.25, bias=half[:]
+                out=logs[:, j, :width], in_=both[:, j, :width], func=ACT.Ln, scale=0.25, bias=half[:]
             )
 
+        z_banks = transpose_z(0)
+        for h in range(HEADS):
+            square_z(0, h)
+        root_z(0)
+        move_z(0, 0, z_banks[0])
+        move_z(0, 1, z_banks[1])
         x_t0 = transpose_x(0)
         x_t1 = transpose_x(1)
         nc.vector.tensor_copy(out=x_grouped[:, 0:2].bitcast(F32), in_=x_t0[:].rearrange("p a u m -> p a m u"))
         nc.scalar.copy(out=x_grouped[:, 2:4].bitcast(F32), in_=x_t1[:].rearrange("p a u m -> p a m u"))
         quantise_half(x_grouped, x_codes, x_scales, 0)
+        quantise_z(0)
         quantise_half(x_grouped, x_codes, x_scales, 1)
-        z_banks = transpose_z(0)
+        z_banks = transpose_z(1)
         xe_banks = [embed(a) for a in range(TILES)]
-        square_z(0, 0)
-        square_z(0, 1)
-        move_z(0, 0, z_banks[0])
+        square_z(1, 0)
+        square_z(1, 1)
+        move_z(1, 0, z_banks[0])
         for a in range(TILES):
             copy = nc.vector.tensor_copy if a % 2 == 0 else nc.scalar.copy
             copy(
@@ -221,46 +244,64 @@ def tile_affnet_kernel(tc, X, W_words, W_scales, Z, beta, out):
                 in_=xe_banks[a][:].rearrange("p (u q c) -> p u c q", u=2, c=2),
             )
         xe_t0 = transpose_xe(0)
-        move_z(0, 1, z_banks[1])
-        square_z(0, 2)
         xe_t1 = transpose_xe(1)
+        move_z(1, 1, z_banks[1])
+        quantise_z(1)
+        square_z(1, 2)
+        square_z(1, 3)
+        root_z(1)
         nc.vector.tensor_copy(out=xe_grouped[:, 0:2], in_=xe_t0[:].rearrange("p a t m -> p a m t"))
         nc.scalar.copy(out=xe_grouped[:, 2:4], in_=xe_t1[:].rearrange("p a t m -> p a m t"))
         xe_banks = [embed(a) for a in range(TILES)]
-        z_banks = transpose_z(1)
-        quantise_z(0)
+        invert_z_norm(0)
         quantise_half(xe_grouped, xe_codes, xe_scales, 0)
         quantise_half(xe_grouped, xe_codes, xe_scales, 1)
-        square_z(0, 3)
-        nc.gpsimd.tensor_tensor(out=z_root[:, 0], in0=z_sumsq[:, 0], in1=root[:], op=ALU.pow)
         for a in range(TILES):
             squares_x = work.tile([P, EMBED], BF16)
             nc.scalar.activation(
                 out=squares_x[:], in_=xe_banks[a][:], func=ACT.Square, accum_out=x_sumsq[:, a : a + 1]
             )
         nc.gpsimd.tensor_tensor(out=x_root[:], in0=x_sumsq[:], in1=root[:], op=ALU.pow)
-        nc.vector.tensor_scalar_add(out=z_norm[:, 0], in0=z_root[:, 0], scalar1=EPS)
-        nc.vector.reciprocal(out=z_inv[:, 0], in_=z_norm[:, 0])
+        for j in range(2, TILES):
+            z_banks = transpose_z(j)
+            move_z(j, 0, z_banks[0])
+            move_z(j, 1, z_banks[1])
+            if j == 2:
+                quantise_z(2)
+        nc.vector.tensor_scalar_add(out=x_norm[:], in0=x_root[:], scalar1=EPS)
+        nc.vector.reciprocal(out=x_inv[:], in_=x_norm[:])
+        nc.vector.tensor_copy(out=beta_f[:], in_=beta_b[:])
+        quantise_z(3)
+        square_z(2, 0)
+        square_z(2, 1)
         aff_banks = multiply(0)
+        row_ps = psum_t.tile([P, NODES], F32, tag="t")
+        for a in range(TILES):
+            nc.tensor.matmul(
+                out=row_ps[:, a * P : (a + 1) * P],
+                lhsT=x_inv[:, a : a + 1].to_broadcast([P, P]),
+                rhs=ident_f[:],
+                start=True,
+                stop=True,
+            )
 
-        pending = None
+        flipped = []
         for j in range(TILES):
             first = work.tile([P, NODES], F32, name="running", bufs=4)
             nc.scalar.activation(out=first[:], in_=aff_banks[0][:], func=ACT.Copy, scale=z_inv[:, j, 0:1])
-            if j + 1 < TILES:
-                move_z(j + 1, 0, z_banks[0])
-                move_z(j + 1, 1, z_banks[1])
-                for h in range(HEADS):
-                    square_z(j + 1, h)
-                nc.gpsimd.tensor_tensor(
-                    out=z_root[:, j + 1], in0=z_sumsq[:, j + 1], in1=root[:], op=ALU.pow
-                )
-            if j + 2 < TILES:
-                z_banks = transpose_z(j + 2)
-            if pending is not None:
-                symmetrise(j - 1, pending[0], pending[1])
-            if j + 1 < TILES:
-                quantise_z(j + 1)
+            if j == 0:
+                square_z(2, 2)
+                square_z(2, 3)
+                root_z(2)
+                square_z(3, 0)
+                square_z(3, 1)
+            if j == 1:
+                nc.scalar.copy(out=x_inv_row[:], in_=row_ps[:])
+                square_z(3, 2)
+                square_z(3, 3)
+                root_z(3)
+            if j > 0:
+                scale_columns(j - 1)
             running = first[:]
             for h in range(1, HEADS):
                 if h == HEADS - 1:
@@ -272,27 +313,15 @@ def tile_affnet_kernel(tc, X, W_words, W_scales, Z, beta, out):
                     op0=ALU.mult, op1=ALU.max,
                 )
                 running = larger
+                if h == 1 and j + 1 < TILES:
+                    invert_z_norm(j + 1)
             if j + 1 < TILES:
                 aff_banks = multiply(j + 1)
-                nc.vector.tensor_scalar_add(out=z_norm[:, j + 1], in0=z_root[:, j + 1], scalar1=EPS)
-                nc.vector.reciprocal(out=z_inv[:, j + 1], in_=z_norm[:, j + 1])
-            if j == 0:
-                nc.vector.tensor_scalar_add(out=x_norm[:], in0=x_root[:], scalar1=EPS)
-                nc.vector.reciprocal(out=x_inv[:], in_=x_norm[:])
-                nc.vector.tensor_copy(out=beta_f[:], in_=beta_b[:])
-                row_ps = psum_t.tile([P, NODES], F32, tag="t")
-                for a in range(TILES):
-                    nc.tensor.matmul(
-                        out=row_ps[:, a * P : (a + 1) * P],
-                        lhsT=x_inv[:, a : a + 1].to_broadcast([P, P]),
-                        rhs=ident_f[:],
-                        start=True,
-                        stop=True,
-                    )
-                nc.scalar.copy(out=x_inv_row[:], in_=row_ps[:])
-            pending = flip(j)
-        symmetrise(TILES - 1, pending[0], pending[1])
+            flipped.append(flip(j))
+        scale_columns(TILES - 1)
 
+        for j in range(TILES):
+            symmetrise(j, flipped[j])
         mirrors = [psum_t.tile([P, NODES], F32, name="mirror%d" % i, tag="t") for i in range(TILES - 1)]
         for j in reversed(range(TILES)):
             width = (j + 1) * P

@@ -20,6 +20,7 @@ FEATURES = 512
 EMBED = 512
 HEADS = 4
 TILES = NODES // P
+LAST = TILES - 1
 EPS = 1e-6
 
 FLOPS = 2 * NODES * FEATURES * EMBED + 2 * HEADS * NODES * NODES * EMBED
@@ -36,6 +37,7 @@ def tile_affnet_kernel(tc, X, W_words, W_scales, Z, beta, out):
 
         w_plane = keep.tile([P, EMBED], U8, align_bytes=64)
         nc.vector.memset(w_plane[:].bitcast(I32), 0)
+        w_plane_t = keep.tile([P, EMBED], U8, align_bytes=64)
         half = keep.tile([P, 1], F32)
         nc.vector.memset(half[:], 0.5)
         root = keep.tile([P, HEADS], F32)
@@ -44,39 +46,38 @@ def tile_affnet_kernel(tc, X, W_words, W_scales, Z, beta, out):
         nc.scalar.activation(out=warm[:], in_=half[:], func=ACT.Ln)
         ident_f = keep.tile([P, P], F32)
         make_identity(nc, ident_f[:])
-        ident_b = keep.tile([P, P], BF16)
-        make_identity(nc, ident_b[:])
 
         z_sb = keep.tile([P, TILES, HEADS, EMBED], BF16)
         x_sb = keep.tile([P, TILES, FEATURES], BF16)
         w_words = keep.tile([P, 2 * EMBED], U8, align_bytes=64)
+        w_words_t = keep.tile([P, 2 * EMBED], U8, align_bytes=64)
         beta_b = keep.tile([P, 1], BF16)
 
-        def load_z(j):
-            for hb in range(2):
-                nc.sync.dma_start(
-                    out=z_sb[:, j, 2 * hb : 2 * hb + 2, :],
-                    in_=Z[2 * hb : 2 * hb + 2, j * P : (j + 1) * P, :].rearrange("h p e -> p h e"),
-                )
+        def load_z(j, hb):
+            nc.sync.dma_start(
+                out=z_sb[:, j, 2 * hb : 2 * hb + 2, :],
+                in_=Z[2 * hb : 2 * hb + 2, j * P : (j + 1) * P, :].rearrange("h p e -> p h e"),
+            )
 
-        load_z(0)
         x_rows = X.rearrange("(a p) f -> p a f", p=P)
-        for b in range(2):
-            nc.sync.dma_start(out=x_sb[:, 2 * b : 2 * b + 2, :], in_=x_rows[:, 2 * b : 2 * b + 2, :])
+        nc.sync.dma_start(out=x_sb[:, 0:2, :], in_=x_rows[:, 0:2, :])
+        nc.sync.dma_start(out=w_words[:].bitcast(I32), in_=W_words[0].bitcast(I32))
         for q in range(4):
             nc.sync.dma_start(
                 out=w_plane[32 * q : 32 * q + 4, :].bitcast(I32),
                 in_=W_scales[0, 4 * q : 4 * q + 4, :].bitcast(I32),
             )
-        nc.sync.dma_start(out=w_words[:].bitcast(I32), in_=W_words[0].bitcast(I32))
+        nc.sync.dma_start(out=x_sb[:, 2:4, :], in_=x_rows[:, 2:4, :])
+        load_z(0, 0)
+        load_z(0, 1)
         for j in range(1, TILES):
-            load_z(j)
+            for hb in range(2):
+                load_z(j, hb)
         nc.sync.dma_start(out=beta_b[:], in_=beta.partition_broadcast(P))
 
         x_grouped = keep.tile([P, TILES, P, PACK], BF16, align_bytes=64)
         x_codes = keep.tile([P, NODES], U32, align_bytes=64)
         x_scales = keep.tile([P, NODES], U8, align_bytes=64)
-        xe_bf = keep.tile([P, TILES, PACK, P], BF16)
         xe_grouped = keep.tile([P, TILES, P, PACK], BF16, align_bytes=64)
         xe_codes = keep.tile([P, NODES], U32, align_bytes=64)
         xe_scales = keep.tile([P, NODES], U8, align_bytes=64)
@@ -94,10 +95,22 @@ def tile_affnet_kernel(tc, X, W_words, W_scales, Z, beta, out):
         z_inv = keep.tile([P, TILES, HEADS], F32)
         best = keep.tile([P, TILES, NODES], F32)
         direct = keep.tile([P, TILES, NODES], F32)
-        both = keep.tile([P, TILES, NODES], F32)
+        both = keep.tile([P, LAST, NODES], F32)
+        late = keep.tile([P, TILES, P], F32)
         logs = keep.tile([P, TILES, NODES], F32)
         result = keep.tile([P, TILES, NODES], F32)
         beta_f = keep.tile([P, 1], F32)
+
+        def permute_w():
+            for u in range(2):
+                nc.vector.tensor_copy(
+                    out=w_words_t[:, u * EMBED : (u + 1) * EMBED].rearrange("p (c q b) -> p q c b", c=2, b=2),
+                    in_=w_words[:, u * EMBED : (u + 1) * EMBED].rearrange("p (q c b) -> p q c b", c=2, b=2),
+                )
+            nc.vector.tensor_copy(
+                out=w_plane_t[:].rearrange("p (u c q) -> p u q c", u=2, c=2),
+                in_=w_plane[:].rearrange("p (u q c) -> p u q c", u=2, c=2),
+            )
 
         def transpose_x(b):
             x_t = psum_t.tile([P, 2, 2, P], F32, tag="t")
@@ -110,16 +123,46 @@ def tile_affnet_kernel(tc, X, W_words, W_scales, Z, beta, out):
                     )
             return x_t
 
-        def quantise_half(grouped, codes, scales, b):
+        def move_x(copy, b, x_t):
+            copy(
+                out=x_grouped[:, 2 * b : 2 * b + 2].bitcast(F32),
+                in_=x_t[:].rearrange("p a u m -> p a m u"),
+            )
+
+        def quantise_x(b):
             cols = slice(2 * b * P, (2 * b + 2) * P)
             nc.vector.quantize_mx(
-                out=codes[:, cols].bitcast(FP8X4),
-                scales=scales[:, cols],
-                in_=grouped[:, 2 * b : 2 * b + 2].rearrange("p a m t -> p (a m t)"),
+                out=x_codes[:, cols].bitcast(FP8X4),
+                scales=x_scales[:, cols],
+                in_=x_grouped[:, 2 * b : 2 * b + 2].rearrange("p a m t -> p (a m t)"),
+            )
+
+        def embed_t(a):
+            xe_t = psum_m.tile([P, PACK, P], F32, tag="m")
+            for t in range(PACK):
+                nc.tensor.matmul_mx(
+                    out=xe_t[:, t, :],
+                    lhsT=w_words_t[:, 2 * P * t : 2 * P * (t + 1)].bitcast(FP4X4),
+                    lhsT_scale=w_plane_t[:, P * t : P * (t + 1)],
+                    rhs=x_codes[:, a * P : (a + 1) * P].bitcast(FP8X4),
+                    rhs_scale=x_scales[:, a * P : (a + 1) * P],
+                    start=True,
+                    stop=True,
+                )
+            return xe_t
+
+        def round_xe(copy, a, xe_t):
+            copy(out=xe_grouped[:, a], in_=xe_t[:].rearrange("p t n -> p n t"))
+
+        def quantise_xe():
+            nc.vector.quantize_mx(
+                out=xe_codes[:].bitcast(FP8X4),
+                scales=xe_scales[:],
+                in_=xe_grouped[:].rearrange("p a m t -> p (a m t)"),
             )
 
         def embed(a):
-            xe_ps = psum_m.tile([P, EMBED], F32, tag="m")
+            xe_ps = psum_t.tile([P, EMBED], F32, tag="t")
             nc.tensor.matmul_mx(
                 out=xe_ps[:],
                 lhsT=x_codes[:, a * P : (a + 1) * P].bitcast(FP8X4),
@@ -131,29 +174,25 @@ def tile_affnet_kernel(tc, X, W_words, W_scales, Z, beta, out):
             )
             return xe_ps
 
-        def transpose_xe(b):
-            xe_t = psum_t.tile([P, 2, PACK, P], BF16, tag="t")
-            for a in range(2):
-                for t in range(PACK):
-                    nc.tensor.transpose(xe_t[:, a, t, :], xe_bf[:, 2 * b + a, t, :], ident_b[:])
-            return xe_t
+        def square_x(a, xe_ps):
+            squares = work.tile([P, EMBED], BF16)
+            nc.scalar.activation(
+                out=squares[:], in_=xe_ps[:], func=ACT.Square, accum_out=x_sumsq[:, a : a + 1]
+            )
 
-        def transpose_z(j):
-            banks = []
-            for hb in range(2):
-                z_t = psum_t.tile([P, 2, 2, P], F32, tag="t")
-                for h in range(2):
-                    for u in range(2):
-                        nc.tensor.transpose(
-                            z_t[:, h, u, :],
-                            z_sb[:, j, 2 * hb + h, :].bitcast(F32)[:, u * P : (u + 1) * P],
-                            ident_f[:],
-                        )
-                banks.append(z_t)
-            return banks
+        def transpose_z(j, hb):
+            z_t = psum_t.tile([P, 2, 2, P], F32, tag="t")
+            for h in range(2):
+                for u in range(2):
+                    nc.tensor.transpose(
+                        z_t[:, h, u, :],
+                        z_sb[:, j, 2 * hb + h, :].bitcast(F32)[:, u * P : (u + 1) * P],
+                        ident_f[:],
+                    )
+            return z_t
 
-        def move_z(j, hb, z_t):
-            nc.vector.tensor_copy(
+        def move_z(copy, j, hb, z_t):
+            copy(
                 out=z_grouped[:, j, 2 * hb : 2 * hb + 2].bitcast(F32),
                 in_=z_t[:].rearrange("p h u n -> p h n u"),
             )
@@ -172,6 +211,25 @@ def tile_affnet_kernel(tc, X, W_words, W_scales, Z, beta, out):
                 in_=z_grouped[:, j].rearrange("p h n t -> p (h n t)"),
             )
 
+        def square_z_on_vector(j, h):
+            squares = work.tile([P, EMBED], BF16)
+            nc.vector.scalar_tensor_tensor(
+                out=squares[:], in0=z_sb[:, j, h, :], scalar=1.0, in1=z_sb[:, j, h, :],
+                op0=ALU.mult, op1=ALU.mult, accum_out=z_sumsq[:, j, h : h + 1],
+            )
+
+        def root_z(j, hb):
+            pair = slice(2 * hb, 2 * hb + 2)
+            nc.gpsimd.tensor_tensor(
+                out=z_root[:, j, pair], in0=z_sumsq[:, j, pair], in1=root[:, :2], op=ALU.pow
+            )
+
+        def add_eps_z(j, pair):
+            nc.vector.tensor_scalar_add(out=z_norm[:, j, pair], in0=z_root[:, j, pair], scalar1=EPS)
+
+        def invert_z_norm(j, pair):
+            nc.vector.reciprocal(out=z_inv[:, j, pair], in_=z_norm[:, j, pair])
+
         def multiply(j):
             banks = []
             for h in range(HEADS):
@@ -188,93 +246,134 @@ def tile_affnet_kernel(tc, X, W_words, W_scales, Z, beta, out):
                 banks.append(aff_ps)
             return banks
 
-        def invert_z_norm(j):
-            nc.vector.tensor_scalar_add(out=z_norm[:, j], in0=z_root[:, j], scalar1=EPS)
-            nc.vector.reciprocal(out=z_inv[:, j], in_=z_norm[:, j])
+        def scale_head_0(j, banks):
+            first = work.tile([P, NODES], F32, name="running", bufs=4)
+            nc.scalar.activation(out=first[:], in_=banks[0][:], func=ACT.Copy, scale=z_inv[:, j, 0:1])
+            return first
 
-        def root_z(j):
-            nc.gpsimd.tensor_tensor(out=z_root[:, j], in0=z_sumsq[:, j], in1=root[:], op=ALU.pow)
+        def keep_larger(j, h, banks, running):
+            if h == HEADS - 1:
+                larger = best[:, j, :]
+            else:
+                larger = work.tile([P, NODES], F32, name="running", bufs=4)[:]
+            nc.vector.scalar_tensor_tensor(
+                out=larger, in0=banks[h][:], scalar=z_inv[:, j, h : h + 1], in1=running,
+                op0=ALU.mult, op1=ALU.max,
+            )
+            return larger
 
-        def flip(j):
-            flipped = psum_t.tile([P, NODES], F32, tag="t")
-            for i in range(j + 1):
-                nc.tensor.transpose(
-                    flipped[:, i * P : (i + 1) * P], best[:, i, j * P : (j + 1) * P], ident_f[:]
-                )
-            return flipped
+        def keep_larger_half(j, h, banks, running, half_cols, larger):
+            nc.vector.scalar_tensor_tensor(
+                out=larger[:, half_cols], in0=banks[h][:, half_cols], scalar=z_inv[:, j, h : h + 1],
+                in1=running[:, half_cols], op0=ALU.mult, op1=ALU.max,
+            )
 
-        def scale_columns(j):
-            width = (j + 1) * P
+        def scale_columns(j, blocks):
+            cols = slice(blocks[0] * P, (blocks[-1] + 1) * P)
             nc.gpsimd.tensor_tensor(
-                out=direct[:, j, :width], in0=best[:, j, :width], in1=x_inv_row[:, :width], op=ALU.mult
+                out=direct[:, j, cols], in0=best[:, j, cols], in1=x_inv_row[:, cols], op=ALU.mult
             )
 
         def symmetrise(j, flipped):
             width = (j + 1) * P
             nc.vector.scalar_tensor_tensor(
-                out=both[:, j, :width], in0=flipped[:, :width], scalar=x_inv[:, j : j + 1],
+                out=both[:, j, :width], in0=flipped, scalar=x_inv[:, j : j + 1],
                 in1=direct[:, j, :width], op0=ALU.mult, op1=ALU.add,
             )
-            nc.scalar.activation(
-                out=logs[:, j, :width], in_=both[:, j, :width], func=ACT.Ln, scale=0.25, bias=half[:]
-            )
 
-        z_banks = transpose_z(0)
-        for h in range(HEADS):
-            square_z(0, h)
-        root_z(0)
-        move_z(0, 0, z_banks[0])
-        move_z(0, 1, z_banks[1])
+        def log(out_ap, in_ap):
+            nc.scalar.activation(out=out_ap, in_=in_ap, func=ACT.Ln, scale=0.25, bias=half[:])
+
+        def power(out_ap, in_ap):
+            nc.scalar.activation(out=out_ap, in_=in_ap, func=ACT.Exp, scale=beta_f[:])
+
+        on_vector = nc.vector.tensor_copy
+        on_scalar = nc.scalar.copy
+
+        ALL, LOW, HIGH = slice(0, 4), slice(0, 2), slice(2, 4)
         x_t0 = transpose_x(0)
+        permute_w()
+        move_x(on_vector, 0, x_t0)
         x_t1 = transpose_x(1)
-        nc.vector.tensor_copy(out=x_grouped[:, 0:2].bitcast(F32), in_=x_t0[:].rearrange("p a u m -> p a m u"))
-        nc.scalar.copy(out=x_grouped[:, 2:4].bitcast(F32), in_=x_t1[:].rearrange("p a u m -> p a m u"))
-        quantise_half(x_grouped, x_codes, x_scales, 0)
+        square_z(0, 0)
+        move_x(on_scalar, 1, x_t1)
+        z_t0 = transpose_z(0, 0)
+        quantise_x(0)
+        xe_banks = [embed_t(0), embed_t(1)]
+        z_t1 = transpose_z(0, 1)
+        move_z(on_vector, 0, 0, z_t0)
+        quantise_x(1)
+        xe_banks += [embed_t(2), embed_t(3)]
+        square_z(0, 1)
+        root_z(0, 0)
+        square_z(0, 2)
+        round_xe(on_vector, 0, xe_banks[0])
+        round_xe(on_scalar, 1, xe_banks[1])
+        move_z(on_vector, 0, 1, z_t1)
+        square_z(0, 3)
+        root_z(0, 1)
+        round_xe(on_vector, 2, xe_banks[2])
+        round_xe(on_scalar, 3, xe_banks[3])
+        z_t0 = transpose_z(1, 0)
+        z_t1 = transpose_z(1, 1)
         quantise_z(0)
-        quantise_half(x_grouped, x_codes, x_scales, 1)
-        z_banks = transpose_z(1)
-        xe_banks = [embed(a) for a in range(TILES)]
+        add_eps_z(0, ALL)
+        quantise_xe()
+        invert_z_norm(0, ALL)
         square_z(1, 0)
         square_z(1, 1)
-        move_z(1, 0, z_banks[0])
-        for a in range(TILES):
-            copy = nc.vector.tensor_copy if a % 2 == 0 else nc.scalar.copy
-            copy(
-                out=xe_bf[:, a].rearrange("p (u c) q -> p u c q", u=2),
-                in_=xe_banks[a][:].rearrange("p (u q c) -> p u c q", u=2, c=2),
-            )
-        xe_t0 = transpose_xe(0)
-        xe_t1 = transpose_xe(1)
-        move_z(1, 1, z_banks[1])
-        quantise_z(1)
+        root_z(1, 0)
         square_z(1, 2)
-        square_z(1, 3)
-        root_z(1)
-        nc.vector.tensor_copy(out=xe_grouped[:, 0:2], in_=xe_t0[:].rearrange("p a t m -> p a m t"))
-        nc.scalar.copy(out=xe_grouped[:, 2:4], in_=xe_t1[:].rearrange("p a t m -> p a m t"))
-        xe_banks = [embed(a) for a in range(TILES)]
-        invert_z_norm(0)
-        quantise_half(xe_grouped, xe_codes, xe_scales, 0)
-        quantise_half(xe_grouped, xe_codes, xe_scales, 1)
-        for a in range(TILES):
-            squares_x = work.tile([P, EMBED], BF16)
-            nc.scalar.activation(
-                out=squares_x[:], in_=xe_banks[a][:], func=ACT.Square, accum_out=x_sumsq[:, a : a + 1]
-            )
-        nc.gpsimd.tensor_tensor(out=x_root[:], in0=x_sumsq[:], in1=root[:], op=ALU.pow)
-        for j in range(2, TILES):
-            z_banks = transpose_z(j)
-            move_z(j, 0, z_banks[0])
-            move_z(j, 1, z_banks[1])
-            if j == 2:
-                quantise_z(2)
-        nc.vector.tensor_scalar_add(out=x_norm[:], in0=x_root[:], scalar1=EPS)
-        nc.vector.reciprocal(out=x_inv[:], in_=x_norm[:])
-        nc.vector.tensor_copy(out=beta_f[:], in_=beta_b[:])
-        quantise_z(3)
+        norm_banks = [embed(0), embed(1)]
+        square_x(0, norm_banks[0])
+        aff = multiply(0)
+        move_z(on_vector, 1, 0, z_t0)
+        first = scale_head_0(0, aff)
+        move_z(on_vector, 1, 1, z_t1)
+        square_z_on_vector(1, 3)
+        root_z(1, 1)
+        z_t0 = transpose_z(2, 0)
+        z_t1 = transpose_z(2, 1)
+        square_x(1, norm_banks[1])
+        norm_banks = [embed(2), embed(3)]
         square_z(2, 0)
         square_z(2, 1)
-        aff_banks = multiply(0)
+        root_z(2, 0)
+
+        running = keep_larger(0, 1, aff, first[:])
+        quantise_z(1)
+        running = keep_larger(0, 2, aff, running)
+        add_eps_z(1, ALL)
+        move_z(on_vector, 2, 0, z_t0)
+        invert_z_norm(1, ALL)
+        running = keep_larger(0, 3, aff, running)
+        move_z(on_vector, 2, 1, z_t1)
+        aff = multiply(1)
+        square_x(2, norm_banks[0])
+        first = scale_head_0(1, aff)
+        square_x(3, norm_banks[1])
+        nc.gpsimd.tensor_tensor(out=x_root[:], in0=x_sumsq[:], in1=root[:], op=ALU.pow)
+        z_t0 = transpose_z(3, 0)
+        z_t1 = transpose_z(3, 1)
+        square_z(2, 2)
+        square_z(2, 3)
+        root_z(2, 1)
+        square_z(3, 0)
+        square_z(3, 1)
+        root_z(3, 0)
+        running = keep_larger(1, 1, aff, first[:])
+        quantise_z(2)
+        running = keep_larger(1, 2, aff, running)
+        add_eps_z(2, LOW)
+        move_z(on_vector, 3, 0, z_t0)
+        invert_z_norm(2, LOW)
+        nc.vector.tensor_scalar_add(out=x_norm[:], in0=x_root[:], scalar1=EPS)
+        running = keep_larger(1, 3, aff, running)
+        nc.vector.reciprocal(out=x_inv[:], in_=x_norm[:])
+        move_z(on_vector, 3, 1, z_t1)
+        add_eps_z(2, HIGH)
+        aff = multiply(2)
+        first = scale_head_0(2, aff)
         row_ps = psum_t.tile([P, NODES], F32, tag="t")
         for a in range(TILES):
             nc.tensor.matmul(
@@ -284,54 +383,87 @@ def tile_affnet_kernel(tc, X, W_words, W_scales, Z, beta, out):
                 start=True,
                 stop=True,
             )
+        square_z(3, 2)
+        square_z(3, 3)
+        root_z(3, 1)
+        nc.scalar.copy(out=x_inv_row[:], in_=row_ps[:])
+        flip_a = psum_t.tile([P, TILES, P], F32, tag="t")
+        flip_b = psum_t.tile([P, 2, P], F32, tag="t")
+        nc.tensor.transpose(flip_a[:, 0, :], best[:, 0, 0:P], ident_f[:])
+        for i in range(2):
+            nc.tensor.transpose(flip_b[:, i, :], best[:, i, P : 2 * P], ident_f[:])
+        scale_columns(0, (0,))
+        scale_columns(1, (0, 1))
+        halves = (slice(0, NODES // 2), slice(NODES // 2, NODES))
 
-        flipped = []
-        for j in range(TILES):
-            first = work.tile([P, NODES], F32, name="running", bufs=4)
-            nc.scalar.activation(out=first[:], in_=aff_banks[0][:], func=ACT.Copy, scale=z_inv[:, j, 0:1])
-            if j == 0:
-                square_z(2, 2)
-                square_z(2, 3)
-                root_z(2)
-                square_z(3, 0)
-                square_z(3, 1)
-            if j == 1:
-                nc.scalar.copy(out=x_inv_row[:], in_=row_ps[:])
-                square_z(3, 2)
-                square_z(3, 3)
-                root_z(3)
-            if j > 0:
-                scale_columns(j - 1)
-            running = first[:]
-            for h in range(1, HEADS):
-                if h == HEADS - 1:
-                    larger = best[:, j, :]
-                else:
-                    larger = work.tile([P, NODES], F32, name="running", bufs=4)[:]
-                nc.vector.scalar_tensor_tensor(
-                    out=larger, in0=aff_banks[h][:], scalar=z_inv[:, j, h : h + 1], in1=running,
-                    op0=ALU.mult, op1=ALU.max,
-                )
-                running = larger
-                if h == 1 and j + 1 < TILES:
-                    invert_z_norm(j + 1)
-            if j + 1 < TILES:
-                aff_banks = multiply(j + 1)
-            flipped.append(flip(j))
-        scale_columns(TILES - 1)
+        def keep_larger_halves(j, h, banks, running):
+            if h == HEADS - 1:
+                larger = best[:, j, :]
+            else:
+                larger = work.tile([P, NODES], F32, name="running", bufs=4)[:]
+            for cols in halves:
+                keep_larger_half(j, h, banks, running, cols, larger)
+            return larger
 
-        for j in range(TILES):
-            symmetrise(j, flipped[j])
-        mirrors = [psum_t.tile([P, NODES], F32, name="mirror%d" % i, tag="t") for i in range(TILES - 1)]
-        for j in reversed(range(TILES)):
-            width = (j + 1) * P
-            nc.scalar.activation(
-                out=result[:, j, :width], in_=logs[:, j, :width], func=ACT.Exp, scale=beta_f[:]
-            )
-            for i in range(j):
+        running = keep_larger(2, 1, aff, first[:])
+        invert_z_norm(2, HIGH)
+        add_eps_z(3, LOW)
+        quantise_z(3)
+        invert_z_norm(3, LOW)
+        running = keep_larger_halves(2, 2, aff, running)
+        running = keep_larger_halves(2, 3, aff, running)
+        aff = multiply(3)
+        nc.vector.tensor_copy(out=beta_f[:], in_=beta_b[:])
+        add_eps_z(3, HIGH)
+        symmetrise(0, flip_a[:, 0, :])
+        invert_z_norm(3, HIGH)
+        first = scale_head_0(3, aff)[:]
+        log(logs[:, 0, :P], both[:, 0, :P])
+        for i in range(3):
+            nc.tensor.transpose(flip_a[:, 1 + i, :], best[:, i, 2 * P : 3 * P], ident_f[:])
+        scale_columns(2, (0, 1, 2, 3))
+        scale_columns(0, (3,))
+        scale_columns(1, (3,))
+        running = keep_larger_halves(3, 1, aff, first)
+        symmetrise(1, flip_b[:].rearrange("p i n -> p (i n)"))
+        log(logs[:, 1, : 2 * P], both[:, 1, : 2 * P])
+        running = keep_larger_halves(3, 2, aff, running)
+        symmetrise(2, flip_a[:, 1:, :].rearrange("p i n -> p (i n)"))
+        log(logs[:, 2, : 3 * P], both[:, 2, : 3 * P])
+        running = keep_larger_halves(3, 3, aff, running)
+
+        late_banks = []
+        for b in range(2):
+            flip_c = psum_m.tile([P, 2, P], F32, tag="m")
+            for i in range(2):
                 nc.tensor.transpose(
-                    mirrors[i][:, j * P : (j + 1) * P], result[:, j, i * P : (i + 1) * P], ident_f[:]
+                    flip_c[:, i, :], best[:, LAST, (2 * b + i) * P : (2 * b + i + 1) * P], ident_f[:]
                 )
-            if width < NODES:
-                nc.vector.tensor_copy(out=result[:, j, width:], in_=mirrors[j][:, width:])
+            late_banks.append(flip_c)
+        scale_columns(LAST, (LAST,))
+        for b in range(2):
+            for i in range(2):
+                node_tile = 2 * b + i
+                nc.vector.scalar_tensor_tensor(
+                    out=late[:, node_tile, :], in0=late_banks[b][:, i, :],
+                    scalar=x_inv[:, node_tile : node_tile + 1], in1=direct[:, node_tile, LAST * P :],
+                    op0=ALU.mult, op1=ALU.add,
+                )
+            log(logs[:, 2 * b : 2 * b + 2, LAST * P :], late[:, 2 * b : 2 * b + 2, :])
+        mirror_a = psum_m.tile([P, 3, P], F32, tag="m")
+        nc.tensor.transpose(mirror_a[:, 0, :], logs[:, 1, :P], ident_f[:])
+        for i in range(2):
+            nc.tensor.transpose(mirror_a[:, 1 + i, :], logs[:, 2, i * P : (i + 1) * P], ident_f[:])
+        mirror_b = psum_m.tile([P, TILES, P], F32, tag="m")
+        for i in range(TILES):
+            nc.tensor.transpose(mirror_b[:, i, :], logs[:, i, LAST * P :], ident_f[:])
+        nc.vector.tensor_copy(
+            out=logs[:, 0, P : 3 * P], in_=mirror_a[:, 0:2, :].rearrange("p i n -> p (i n)")
+        )
+        nc.vector.tensor_copy(out=logs[:, 1, 2 * P : 3 * P], in_=mirror_a[:, 2, :])
+        for j in (2, 1, 0, 3):
+            if j == LAST:
+                power(result[:, j, :], mirror_b[:].rearrange("p i n -> p (i n)"))
+            else:
+                power(result[:, j, :], logs[:, j, :])
             nc.sync.dma_start(out=out[j * P : (j + 1) * P, :], in_=result[:, j, :])

@@ -204,6 +204,23 @@ def tile_affnet_kernel(tc, X, W_words, W_scales, Z, beta, out):
                 accum_out=z_sumsq[:, j, h : h + 1],
             )
 
+        def gram(j, heads):
+            bank = psum_t.tile([P, HEADS, P], F32, tag="t")
+            for h in heads:
+                for t in range(PACK):
+                    rows = z_grouped[:, j, h].rearrange("p n t -> p t n")[:, t, :]
+                    nc.tensor.matmul(
+                        out=bank[:, h, :], lhsT=rows, rhs=rows, start=(t == 0), stop=(t == PACK - 1)
+                    )
+            return bank
+
+        def add_diagonal(j, h, bank):
+            products = work.tile([P, P], BF16)
+            nc.vector.scalar_tensor_tensor(
+                out=products[:], in0=bank[:, h, :], scalar=1.0, in1=ident_f[:],
+                op0=ALU.mult, op1=ALU.mult, accum_out=z_sumsq[:, j, h : h + 1],
+            )
+
         def quantise_z(j):
             nc.vector.quantize_mx(
                 out=z_codes[:, j, :].bitcast(FP8X4),
@@ -230,9 +247,9 @@ def tile_affnet_kernel(tc, X, W_words, W_scales, Z, beta, out):
         def invert_z_norm(j, pair):
             nc.vector.reciprocal(out=z_inv[:, j, pair], in_=z_norm[:, j, pair])
 
-        def multiply(j):
+        def multiply(j, heads=range(HEADS)):
             banks = []
-            for h in range(HEADS):
+            for h in heads:
                 aff_ps = psum_m.tile([P, NODES], F32, tag="m")
                 nc.tensor.matmul_mx(
                     out=aff_ps[:],
@@ -268,9 +285,9 @@ def tile_affnet_kernel(tc, X, W_words, W_scales, Z, beta, out):
                 in1=running[:, half_cols], op0=ALU.mult, op1=ALU.max,
             )
 
-        def scale_columns(j, blocks):
+        def scale_columns(engine, j, blocks):
             cols = slice(blocks[0] * P, (blocks[-1] + 1) * P)
-            nc.gpsimd.tensor_tensor(
+            engine.tensor_tensor(
                 out=direct[:, j, cols], in0=best[:, j, cols], in1=x_inv_row[:, cols], op=ALU.mult
             )
 
@@ -291,109 +308,6 @@ def tile_affnet_kernel(tc, X, W_words, W_scales, Z, beta, out):
         on_scalar = nc.scalar.copy
 
         ALL, LOW, HIGH = slice(0, 4), slice(0, 2), slice(2, 4)
-        x_t0 = transpose_x(0)
-        permute_w()
-        move_x(on_vector, 0, x_t0)
-        x_t1 = transpose_x(1)
-        square_z(0, 0)
-        move_x(on_scalar, 1, x_t1)
-        z_t0 = transpose_z(0, 0)
-        quantise_x(0)
-        xe_banks = [embed_t(0), embed_t(1)]
-        z_t1 = transpose_z(0, 1)
-        move_z(on_vector, 0, 0, z_t0)
-        quantise_x(1)
-        xe_banks += [embed_t(2), embed_t(3)]
-        square_z(0, 1)
-        root_z(0, 0)
-        square_z(0, 2)
-        round_xe(on_vector, 0, xe_banks[0])
-        round_xe(on_scalar, 1, xe_banks[1])
-        move_z(on_vector, 0, 1, z_t1)
-        square_z(0, 3)
-        root_z(0, 1)
-        round_xe(on_vector, 2, xe_banks[2])
-        round_xe(on_scalar, 3, xe_banks[3])
-        z_t0 = transpose_z(1, 0)
-        z_t1 = transpose_z(1, 1)
-        quantise_z(0)
-        add_eps_z(0, ALL)
-        quantise_xe()
-        invert_z_norm(0, ALL)
-        square_z(1, 0)
-        square_z(1, 1)
-        root_z(1, 0)
-        square_z(1, 2)
-        norm_banks = [embed(0), embed(1)]
-        square_x(0, norm_banks[0])
-        aff = multiply(0)
-        move_z(on_vector, 1, 0, z_t0)
-        first = scale_head_0(0, aff)
-        move_z(on_vector, 1, 1, z_t1)
-        square_z_on_vector(1, 3)
-        root_z(1, 1)
-        z_t0 = transpose_z(2, 0)
-        z_t1 = transpose_z(2, 1)
-        square_x(1, norm_banks[1])
-        norm_banks = [embed(2), embed(3)]
-        square_z(2, 0)
-        square_z(2, 1)
-        root_z(2, 0)
-
-        running = keep_larger(0, 1, aff, first[:])
-        quantise_z(1)
-        running = keep_larger(0, 2, aff, running)
-        add_eps_z(1, ALL)
-        move_z(on_vector, 2, 0, z_t0)
-        invert_z_norm(1, ALL)
-        running = keep_larger(0, 3, aff, running)
-        move_z(on_vector, 2, 1, z_t1)
-        aff = multiply(1)
-        square_x(2, norm_banks[0])
-        first = scale_head_0(1, aff)
-        square_x(3, norm_banks[1])
-        nc.gpsimd.tensor_tensor(out=x_root[:], in0=x_sumsq[:], in1=root[:], op=ALU.pow)
-        z_t0 = transpose_z(3, 0)
-        z_t1 = transpose_z(3, 1)
-        square_z(2, 2)
-        square_z(2, 3)
-        root_z(2, 1)
-        square_z(3, 0)
-        square_z(3, 1)
-        root_z(3, 0)
-        running = keep_larger(1, 1, aff, first[:])
-        quantise_z(2)
-        running = keep_larger(1, 2, aff, running)
-        add_eps_z(2, LOW)
-        move_z(on_vector, 3, 0, z_t0)
-        invert_z_norm(2, LOW)
-        nc.vector.tensor_scalar_add(out=x_norm[:], in0=x_root[:], scalar1=EPS)
-        running = keep_larger(1, 3, aff, running)
-        nc.vector.reciprocal(out=x_inv[:], in_=x_norm[:])
-        move_z(on_vector, 3, 1, z_t1)
-        add_eps_z(2, HIGH)
-        aff = multiply(2)
-        first = scale_head_0(2, aff)
-        row_ps = psum_t.tile([P, NODES], F32, tag="t")
-        for a in range(TILES):
-            nc.tensor.matmul(
-                out=row_ps[:, a * P : (a + 1) * P],
-                lhsT=x_inv[:, a : a + 1].to_broadcast([P, P]),
-                rhs=ident_f[:],
-                start=True,
-                stop=True,
-            )
-        square_z(3, 2)
-        square_z(3, 3)
-        root_z(3, 1)
-        nc.scalar.copy(out=x_inv_row[:], in_=row_ps[:])
-        flip_a = psum_t.tile([P, TILES, P], F32, tag="t")
-        flip_b = psum_t.tile([P, 2, P], F32, tag="t")
-        nc.tensor.transpose(flip_a[:, 0, :], best[:, 0, 0:P], ident_f[:])
-        for i in range(2):
-            nc.tensor.transpose(flip_b[:, i, :], best[:, i, P : 2 * P], ident_f[:])
-        scale_columns(0, (0,))
-        scale_columns(1, (0, 1))
         halves = (slice(0, NODES // 2), slice(NODES // 2, NODES))
 
         def keep_larger_halves(j, h, banks, running):
@@ -405,32 +319,146 @@ def tile_affnet_kernel(tc, X, W_words, W_scales, Z, beta, out):
                 keep_larger_half(j, h, banks, running, cols, larger)
             return larger
 
-        running = keep_larger(2, 1, aff, first[:])
+        x_t0 = transpose_x(0)
+        permute_w()
+        move_x(on_vector, 0, x_t0)
+        x_t1 = transpose_x(1)
+        square_z(0, 0)
+        move_x(on_scalar, 1, x_t1)
+        z_t0 = transpose_z(0, 0)
+        z_t1 = transpose_z(0, 1)
+        quantise_x(0)
+        xe_banks = [embed_t(0), embed_t(1)]
+        square_z(0, 1)
+        root_z(0, 0)
+        move_z(on_scalar, 0, 0, z_t0)
+        quantise_x(1)
+        xe_banks += [embed_t(2), embed_t(3)]
+        move_z(on_scalar, 0, 1, z_t1)
+        round_xe(on_vector, 0, xe_banks[0])
+        round_xe(on_scalar, 1, xe_banks[1])
+        round_xe(on_vector, 2, xe_banks[2])
+        round_xe(on_scalar, 3, xe_banks[3])
+        z_t0 = transpose_z(1, 0)
+        z_t1 = transpose_z(1, 1)
+        square_z(0, 2)
+        square_z(0, 3)
+        root_z(0, 1)
+        quantise_z(0)
+        add_eps_z(0, LOW)
+        quantise_xe()
+        invert_z_norm(0, LOW)
+        z_t2 = transpose_z(2, 0)
+        z_t3 = transpose_z(2, 1)
+        square_z(1, 0)
+        aff = multiply(0)
+        move_z(on_vector, 1, 0, z_t0)
+        move_z(on_vector, 1, 1, z_t1)
+        first = scale_head_0(0, aff)
+        move_z(on_vector, 2, 0, z_t2)
+        add_eps_z(0, HIGH)
+        move_z(on_vector, 2, 1, z_t3)
+        invert_z_norm(0, HIGH)
+        square_z(1, 1)
+        root_z(1, 0)
+        square_z(1, 2)
+        square_z(1, 3)
+        root_z(1, 1)
+        norm_banks = [embed(0), embed(1)]
+        gram_bank = gram(2, range(HEADS))
+        square_x(0, norm_banks[0])
+        square_x(1, norm_banks[1])
+
+        running = keep_larger(0, 1, aff, first[:])
+        quantise_z(1)
+        running = keep_larger_halves(0, 2, aff, running)
+        running = keep_larger_halves(0, 3, aff, running)
+        norm_banks += [embed(2)]
+        aff = multiply(1, (0, 1))
+        norm_banks += [embed(3)]
+        aff += multiply(1, (2, 3))
+        square_x(2, norm_banks[2])
+        add_eps_z(1, ALL)
+        add_diagonal(2, 0, gram_bank)
+        add_diagonal(2, 1, gram_bank)
+        root_z(2, 0)
+        invert_z_norm(1, ALL)
+        first = scale_head_0(1, aff)
+        add_diagonal(2, 2, gram_bank)
+        add_diagonal(2, 3, gram_bank)
+        square_x(3, norm_banks[3])
+        nc.gpsimd.tensor_tensor(out=x_root[:], in0=x_sumsq[:], in1=root[:], op=ALU.pow)
+        root_z(2, 1)
+        z_t0 = transpose_z(3, 0)
+        z_t1 = transpose_z(3, 1)
+        square_z(3, 0)
+        move_z(on_scalar, 3, 0, z_t0)
+        square_z(3, 1)
+        root_z(3, 0)
+        quantise_z(2)
+        running = keep_larger_halves(1, 1, aff, first[:])
+        running = keep_larger_halves(1, 2, aff, running)
+        add_eps_z(2, LOW)
+        move_z(on_vector, 3, 1, z_t1)
+        invert_z_norm(2, LOW)
+        keep_larger_half(1, 3, aff, running, halves[0], best[:, 1, :])
+        nc.vector.tensor_scalar_add(out=x_norm[:], in0=x_root[:], scalar1=EPS)
+        keep_larger_half(1, 3, aff, running, halves[1], best[:, 1, :])
+        nc.vector.reciprocal(out=x_inv[:], in_=x_norm[:])
+        aff = multiply(2, (0, 1, 2))
+        first = scale_head_0(2, aff)
+        row_ps = psum_t.tile([P, NODES], F32, tag="t")
+        for a in range(TILES):
+            nc.tensor.matmul(
+                out=row_ps[:, a * P : (a + 1) * P],
+                lhsT=x_inv[:, a : a + 1].to_broadcast([P, P]),
+                rhs=ident_f[:],
+                start=True,
+                stop=True,
+            )
+        aff += multiply(2, (3,))
+        quantise_z(3)
+        aff3 = multiply(3, (0,))
+        square_z(3, 2)
+        square_z(3, 3)
+        root_z(3, 1)
+        nc.scalar.copy(out=x_inv_row[:], in_=row_ps[:])
+        add_eps_z(2, HIGH)
+        second = work.tile([P, NODES], F32, name="running", bufs=4)[:]
+        keep_larger_half(2, 1, aff, first, halves[0], second)
         invert_z_norm(2, HIGH)
         add_eps_z(3, LOW)
-        quantise_z(3)
+        keep_larger_half(2, 1, aff, first, halves[1], second)
+        running = keep_larger_halves(2, 2, aff, second)
         invert_z_norm(3, LOW)
-        running = keep_larger_halves(2, 2, aff, running)
+        first = scale_head_0(3, aff3)[:]
         running = keep_larger_halves(2, 3, aff, running)
-        aff = multiply(3)
-        nc.vector.tensor_copy(out=beta_f[:], in_=beta_b[:])
-        add_eps_z(3, HIGH)
-        symmetrise(0, flip_a[:, 0, :])
-        invert_z_norm(3, HIGH)
-        first = scale_head_0(3, aff)[:]
-        log(logs[:, 0, :P], both[:, 0, :P])
+        aff3 += multiply(3, (1, 2))
+        flip_a = psum_t.tile([P, TILES, P], F32, tag="t")
+        flip_b = psum_t.tile([P, 2, P], F32, tag="t")
+        nc.tensor.transpose(flip_a[:, 0, :], best[:, 0, 0:P], ident_f[:])
+        for i in range(2):
+            nc.tensor.transpose(flip_b[:, i, :], best[:, i, P : 2 * P], ident_f[:])
+        aff3 += multiply(3, (3,))
         for i in range(3):
             nc.tensor.transpose(flip_a[:, 1 + i, :], best[:, i, 2 * P : 3 * P], ident_f[:])
-        scale_columns(2, (0, 1, 2, 3))
-        scale_columns(0, (3,))
-        scale_columns(1, (3,))
-        running = keep_larger_halves(3, 1, aff, first)
+        scale_columns(nc.gpsimd, 0, (3,))
+        scale_columns(nc.gpsimd, 2, (0, 1, 2, 3))
+        scale_columns(nc.gpsimd, 1, (3,))
+        scale_columns(nc.vector, 0, (0,))
+        scale_columns(nc.vector, 1, (0, 1))
+        add_eps_z(3, HIGH)
+        nc.vector.tensor_copy(out=beta_f[:], in_=beta_b[:])
+        running = keep_larger_halves(3, 1, aff3, first)
+        invert_z_norm(3, HIGH)
+        symmetrise(0, flip_a[:, 0, :])
+        log(logs[:, 0, :P], both[:, 0, :P])
+        running = keep_larger_halves(3, 2, aff3, running)
         symmetrise(1, flip_b[:].rearrange("p i n -> p (i n)"))
         log(logs[:, 1, : 2 * P], both[:, 1, : 2 * P])
-        running = keep_larger_halves(3, 2, aff, running)
+        running = keep_larger_halves(3, 3, aff3, running)
         symmetrise(2, flip_a[:, 1:, :].rearrange("p i n -> p (i n)"))
         log(logs[:, 2, : 3 * P], both[:, 2, : 3 * P])
-        running = keep_larger_halves(3, 3, aff, running)
 
         late_banks = []
         for b in range(2):
@@ -440,7 +468,7 @@ def tile_affnet_kernel(tc, X, W_words, W_scales, Z, beta, out):
                     flip_c[:, i, :], best[:, LAST, (2 * b + i) * P : (2 * b + i + 1) * P], ident_f[:]
                 )
             late_banks.append(flip_c)
-        scale_columns(LAST, (LAST,))
+        scale_columns(nc.gpsimd, LAST, (LAST,))
         for b in range(2):
             for i in range(2):
                 node_tile = 2 * b + i

@@ -35,6 +35,12 @@ def tile_affnet_kernel(tc, X, W_words, W_scales, Z, beta, out):
         psum_m = ctx.enter_context(tc.psum_pool(name="psum_m", bufs=4))
         ctx.enter_context(tc.manual_schedule())
 
+        ones = keep.tile([P, P], F32)
+        nc.vector.memset(ones[:], 1.0)
+        idle_ps = psum_m.tile([P, P], F32, tag="m")
+        for i in range(3):
+            nc.tensor.matmul(out=idle_ps[:], lhsT=ones[:], rhs=ones[:], start=True, stop=True)
+
         w_plane = keep.tile([P, EMBED], U8, align_bytes=64)
         nc.vector.memset(w_plane[:].bitcast(I32), 0)
         w_plane_t = keep.tile([P, EMBED], U8, align_bytes=64)
@@ -101,12 +107,14 @@ def tile_affnet_kernel(tc, X, W_words, W_scales, Z, beta, out):
         result = keep.tile([P, TILES, NODES], F32)
         beta_f = keep.tile([P, 1], F32)
 
-        def permute_w():
+        def permute_words():
             for u in range(2):
                 nc.vector.tensor_copy(
                     out=w_words_t[:, u * EMBED : (u + 1) * EMBED].rearrange("p (c q b) -> p q c b", c=2, b=2),
                     in_=w_words[:, u * EMBED : (u + 1) * EMBED].rearrange("p (q c b) -> p q c b", c=2, b=2),
                 )
+
+        def permute_scales():
             nc.vector.tensor_copy(
                 out=w_plane_t[:].rearrange("p (u c q) -> p u q c", u=2, c=2),
                 in_=w_plane[:].rearrange("p (u q c) -> p u q c", u=2, c=2),
@@ -320,8 +328,9 @@ def tile_affnet_kernel(tc, X, W_words, W_scales, Z, beta, out):
             return larger
 
         x_t0 = transpose_x(0)
-        permute_w()
+        permute_words()
         move_x(on_vector, 0, x_t0)
+        permute_scales()
         x_t1 = transpose_x(1)
         square_z(0, 0)
         move_x(on_scalar, 1, x_t1)
@@ -331,8 +340,8 @@ def tile_affnet_kernel(tc, X, W_words, W_scales, Z, beta, out):
         xe_banks = [embed_t(0), embed_t(1)]
         square_z(0, 1)
         root_z(0, 0)
-        move_z(on_scalar, 0, 0, z_t0)
         quantise_x(1)
+        move_z(on_vector, 0, 0, z_t0)
         xe_banks += [embed_t(2), embed_t(3)]
         move_z(on_scalar, 0, 1, z_t1)
         round_xe(on_vector, 0, xe_banks[0])
@@ -351,6 +360,8 @@ def tile_affnet_kernel(tc, X, W_words, W_scales, Z, beta, out):
         z_t2 = transpose_z(2, 0)
         z_t3 = transpose_z(2, 1)
         square_z(1, 0)
+        square_z(1, 1)
+        root_z(1, 0)
         aff = multiply(0)
         move_z(on_vector, 1, 0, z_t0)
         move_z(on_vector, 1, 1, z_t1)
@@ -359,8 +370,6 @@ def tile_affnet_kernel(tc, X, W_words, W_scales, Z, beta, out):
         add_eps_z(0, HIGH)
         move_z(on_vector, 2, 1, z_t3)
         invert_z_norm(0, HIGH)
-        square_z(1, 1)
-        root_z(1, 0)
         square_z(1, 2)
         square_z(1, 3)
         root_z(1, 1)
@@ -373,36 +382,34 @@ def tile_affnet_kernel(tc, X, W_words, W_scales, Z, beta, out):
         quantise_z(1)
         running = keep_larger_halves(0, 2, aff, running)
         running = keep_larger_halves(0, 3, aff, running)
-        norm_banks += [embed(2)]
-        aff = multiply(1, (0, 1))
-        norm_banks += [embed(3)]
-        aff += multiply(1, (2, 3))
+        norm_banks += [embed(2), embed(3)]
+        aff = multiply(1)
         square_x(2, norm_banks[2])
+        square_x(3, norm_banks[3])
         add_eps_z(1, ALL)
         add_diagonal(2, 0, gram_bank)
         add_diagonal(2, 1, gram_bank)
         root_z(2, 0)
+        nc.gpsimd.tensor_tensor(out=x_root[:], in0=x_sumsq[:], in1=root[:], op=ALU.pow)
         invert_z_norm(1, ALL)
         first = scale_head_0(1, aff)
         add_diagonal(2, 2, gram_bank)
         add_diagonal(2, 3, gram_bank)
-        square_x(3, norm_banks[3])
-        nc.gpsimd.tensor_tensor(out=x_root[:], in0=x_sumsq[:], in1=root[:], op=ALU.pow)
         root_z(2, 1)
         z_t0 = transpose_z(3, 0)
         z_t1 = transpose_z(3, 1)
         square_z(3, 0)
         move_z(on_scalar, 3, 0, z_t0)
+        move_z(on_scalar, 3, 1, z_t1)
         square_z(3, 1)
         root_z(3, 0)
         quantise_z(2)
         running = keep_larger_halves(1, 1, aff, first[:])
         running = keep_larger_halves(1, 2, aff, running)
         add_eps_z(2, LOW)
-        move_z(on_vector, 3, 1, z_t1)
-        invert_z_norm(2, LOW)
         keep_larger_half(1, 3, aff, running, halves[0], best[:, 1, :])
         nc.vector.tensor_scalar_add(out=x_norm[:], in0=x_root[:], scalar1=EPS)
+        invert_z_norm(2, LOW)
         keep_larger_half(1, 3, aff, running, halves[1], best[:, 1, :])
         nc.vector.reciprocal(out=x_inv[:], in_=x_norm[:])
         aff = multiply(2, (0, 1, 2))
@@ -427,8 +434,8 @@ def tile_affnet_kernel(tc, X, W_words, W_scales, Z, beta, out):
         second = work.tile([P, NODES], F32, name="running", bufs=4)[:]
         keep_larger_half(2, 1, aff, first, halves[0], second)
         invert_z_norm(2, HIGH)
-        add_eps_z(3, LOW)
         keep_larger_half(2, 1, aff, first, halves[1], second)
+        add_eps_z(3, LOW)
         running = keep_larger_halves(2, 2, aff, second)
         invert_z_norm(3, LOW)
         first = scale_head_0(3, aff3)[:]

@@ -212,15 +212,12 @@ def tile_affnet_kernel(tc, X, W_words, W_scales, Z, beta, out):
                 accum_out=z_sumsq[:, j, h : h + 1],
             )
 
-        def gram(j, heads):
-            bank = psum_t.tile([P, HEADS, P], F32, tag="t")
-            for h in heads:
-                for t in range(PACK):
-                    rows = z_grouped[:, j, h].rearrange("p n t -> p t n")[:, t, :]
-                    nc.tensor.matmul(
-                        out=bank[:, h, :], lhsT=rows, rhs=rows, start=(t == 0), stop=(t == PACK - 1)
-                    )
-            return bank
+        def gram(j, h, bank):
+            for t in range(PACK):
+                rows = z_grouped[:, j, h].rearrange("p n t -> p t n")[:, t, :]
+                nc.tensor.matmul(
+                    out=bank[:, h, :], lhsT=rows, rhs=rows, start=(t == 0), stop=(t == PACK - 1)
+                )
 
         def add_diagonal(j, h, bank):
             products = work.tile([P, P], BF16)
@@ -370,28 +367,32 @@ def tile_affnet_kernel(tc, X, W_words, W_scales, Z, beta, out):
         add_eps_z(0, HIGH)
         move_z(on_vector, 2, 1, z_t3)
         invert_z_norm(0, HIGH)
+        norm_banks = [embed(0), embed(1)]
         square_z(1, 2)
+        square_x(0, norm_banks[0])
         square_z(1, 3)
         root_z(1, 1)
-        norm_banks = [embed(0), embed(1)]
-        gram_bank = gram(2, range(HEADS))
-        square_x(0, norm_banks[0])
+        gram_bank = psum_t.tile([P, HEADS, P], F32, tag="t")
+        gram(2, 0, gram_bank)
+        gram(2, 1, gram_bank)
+        norm_banks += [embed(2), embed(3)]
+        gram(2, 2, gram_bank)
+        gram(2, 3, gram_bank)
         square_x(1, norm_banks[1])
 
         running = keep_larger(0, 1, aff, first[:])
         quantise_z(1)
         running = keep_larger_halves(0, 2, aff, running)
         running = keep_larger_halves(0, 3, aff, running)
-        norm_banks += [embed(2), embed(3)]
         aff = multiply(1)
         square_x(2, norm_banks[2])
         square_x(3, norm_banks[3])
-        add_eps_z(1, ALL)
+        add_eps_z(1, LOW)
         add_diagonal(2, 0, gram_bank)
         add_diagonal(2, 1, gram_bank)
         root_z(2, 0)
         nc.gpsimd.tensor_tensor(out=x_root[:], in0=x_sumsq[:], in1=root[:], op=ALU.pow)
-        invert_z_norm(1, ALL)
+        invert_z_norm(1, LOW)
         first = scale_head_0(1, aff)
         add_diagonal(2, 2, gram_bank)
         add_diagonal(2, 3, gram_bank)
@@ -403,7 +404,9 @@ def tile_affnet_kernel(tc, X, W_words, W_scales, Z, beta, out):
         move_z(on_scalar, 3, 1, z_t1)
         square_z(3, 1)
         root_z(3, 0)
+        add_eps_z(1, HIGH)
         quantise_z(2)
+        invert_z_norm(1, HIGH)
         running = keep_larger_halves(1, 1, aff, first[:])
         running = keep_larger_halves(1, 2, aff, running)
         add_eps_z(2, LOW)

@@ -381,19 +381,21 @@ def tile_affnet_kernel(tc, X, W_words, W_scales, Z, beta, out):
         square_x(1, norm_banks[1])
 
         running = keep_larger(0, 1, aff, first[:])
+        add_eps_z(1, LOW)
         quantise_z(1)
+        invert_z_norm(1, LOW)
         running = keep_larger_halves(0, 2, aff, running)
         running = keep_larger_halves(0, 3, aff, running)
         aff = multiply(1)
         square_x(2, norm_banks[2])
         square_x(3, norm_banks[3])
-        add_eps_z(1, LOW)
+        nc.gpsimd.tensor_tensor(out=x_root[:], in0=x_sumsq[:], in1=root[:], op=ALU.pow)
+        first = scale_head_0(1, aff)
+        quantise_z(2)
+        add_eps_z(1, HIGH)
         add_diagonal(2, 0, gram_bank)
         add_diagonal(2, 1, gram_bank)
         root_z(2, 0)
-        nc.gpsimd.tensor_tensor(out=x_root[:], in0=x_sumsq[:], in1=root[:], op=ALU.pow)
-        invert_z_norm(1, LOW)
-        first = scale_head_0(1, aff)
         add_diagonal(2, 2, gram_bank)
         add_diagonal(2, 3, gram_bank)
         root_z(2, 1)
@@ -404,17 +406,15 @@ def tile_affnet_kernel(tc, X, W_words, W_scales, Z, beta, out):
         move_z(on_scalar, 3, 1, z_t1)
         square_z(3, 1)
         root_z(3, 0)
-        add_eps_z(1, HIGH)
-        quantise_z(2)
         invert_z_norm(1, HIGH)
         running = keep_larger_halves(1, 1, aff, first[:])
         running = keep_larger_halves(1, 2, aff, running)
-        add_eps_z(2, LOW)
         keep_larger_half(1, 3, aff, running, halves[0], best[:, 1, :])
         nc.vector.tensor_scalar_add(out=x_norm[:], in0=x_root[:], scalar1=EPS)
-        invert_z_norm(2, LOW)
+        add_eps_z(2, LOW)
         keep_larger_half(1, 3, aff, running, halves[1], best[:, 1, :])
         nc.vector.reciprocal(out=x_inv[:], in_=x_norm[:])
+        invert_z_norm(2, LOW)
         aff = multiply(2, (0, 1, 2))
         first = scale_head_0(2, aff)
         row_ps = psum_t.tile([P, NODES], F32, tag="t")
@@ -444,14 +444,14 @@ def tile_affnet_kernel(tc, X, W_words, W_scales, Z, beta, out):
         first = scale_head_0(3, aff3)[:]
         running = keep_larger_halves(2, 3, aff, running)
         aff3 += multiply(3, (1, 2))
-        flip_a = psum_t.tile([P, TILES, P], F32, tag="t")
-        flip_b = psum_t.tile([P, 2, P], F32, tag="t")
-        nc.tensor.transpose(flip_a[:, 0, :], best[:, 0, 0:P], ident_f[:])
+        flip_a = psum_t.tile([P, 3, P], F32, tag="t")
+        flip_b = psum_t.tile([P, 3, P], F32, tag="t")
+        nc.tensor.transpose(flip_b[:, 0, :], best[:, 0, 0:P], ident_f[:])
         for i in range(2):
-            nc.tensor.transpose(flip_b[:, i, :], best[:, i, P : 2 * P], ident_f[:])
+            nc.tensor.transpose(flip_b[:, 1 + i, :], best[:, i, P : 2 * P], ident_f[:])
         aff3 += multiply(3, (3,))
         for i in range(3):
-            nc.tensor.transpose(flip_a[:, 1 + i, :], best[:, i, 2 * P : 3 * P], ident_f[:])
+            nc.tensor.transpose(flip_a[:, i, :], best[:, i, 2 * P : 3 * P], ident_f[:])
         scale_columns(nc.gpsimd, 0, (3,))
         scale_columns(nc.gpsimd, 2, (0, 1, 2, 3))
         scale_columns(nc.gpsimd, 1, (3,))
@@ -461,13 +461,13 @@ def tile_affnet_kernel(tc, X, W_words, W_scales, Z, beta, out):
         nc.vector.tensor_copy(out=beta_f[:], in_=beta_b[:])
         running = keep_larger_halves(3, 1, aff3, first)
         invert_z_norm(3, HIGH)
-        symmetrise(0, flip_a[:, 0, :])
+        symmetrise(0, flip_b[:, 0, :])
         log(logs[:, 0, :P], both[:, 0, :P])
         running = keep_larger_halves(3, 2, aff3, running)
-        symmetrise(1, flip_b[:].rearrange("p i n -> p (i n)"))
+        symmetrise(1, flip_b[:, 1:, :].rearrange("p i n -> p (i n)"))
         log(logs[:, 1, : 2 * P], both[:, 1, : 2 * P])
         running = keep_larger_halves(3, 3, aff3, running)
-        symmetrise(2, flip_a[:, 1:, :].rearrange("p i n -> p (i n)"))
+        symmetrise(2, flip_a[:].rearrange("p i n -> p (i n)"))
         log(logs[:, 2, : 3 * P], both[:, 2, : 3 * P])
 
         late_banks = []

@@ -37,9 +37,13 @@ def tile_affnet_kernel(tc, X, W_words, W_scales, Z, beta, out):
 
         ones = keep.tile([P, P], F32)
         nc.vector.memset(ones[:], 1.0)
-        idle_ps = psum_m.tile([P, P], F32, tag="m")
-        for i in range(3):
-            nc.tensor.matmul(out=idle_ps[:], lhsT=ones[:], rhs=ones[:], start=True, stop=True)
+
+        def keep_busy(times):
+            idle_ps = psum_m.tile([P, P], F32, tag="m")
+            for i in range(times):
+                nc.tensor.matmul(out=idle_ps[:], lhsT=ones[:], rhs=ones[:], start=True, stop=True)
+
+        keep_busy(4)
 
         w_plane = keep.tile([P, EMBED], U8, align_bytes=64)
         nc.vector.memset(w_plane[:].bitcast(I32), 0)
@@ -333,6 +337,7 @@ def tile_affnet_kernel(tc, X, W_words, W_scales, Z, beta, out):
         move_x(on_scalar, 1, x_t1)
         z_t0 = transpose_z(0, 0)
         z_t1 = transpose_z(0, 1)
+        keep_busy(2)
         quantise_x(0)
         xe_banks = [embed_t(0), embed_t(1)]
         square_z(0, 1)
@@ -452,9 +457,11 @@ def tile_affnet_kernel(tc, X, W_words, W_scales, Z, beta, out):
         aff3 += multiply(3, (3,))
         for i in range(3):
             nc.tensor.transpose(flip_a[:, i, :], best[:, i, 2 * P : 3 * P], ident_f[:])
-        scale_columns(nc.gpsimd, 0, (3,))
-        scale_columns(nc.gpsimd, 2, (0, 1, 2, 3))
-        scale_columns(nc.gpsimd, 1, (3,))
+        scale_columns(nc.gpsimd, 2, (0, 1, 2))
+        nc.gpsimd.tensor_tensor(
+            out=direct[:, :LAST, LAST * P :], in0=best[:, :LAST, LAST * P :],
+            in1=x_inv_row[:, LAST * P :].unsqueeze(1).broadcast_to([P, LAST, P]), op=ALU.mult,
+        )
         scale_columns(nc.vector, 0, (0,))
         scale_columns(nc.vector, 1, (0, 1))
         add_eps_z(3, HIGH)
@@ -478,7 +485,7 @@ def tile_affnet_kernel(tc, X, W_words, W_scales, Z, beta, out):
                     flip_c[:, i, :], best[:, LAST, (2 * b + i) * P : (2 * b + i + 1) * P], ident_f[:]
                 )
             late_banks.append(flip_c)
-        scale_columns(nc.gpsimd, LAST, (LAST,))
+        scale_columns(nc.vector, LAST, (LAST,))
         for b in range(2):
             for i in range(2):
                 node_tile = 2 * b + i

from contextlib import ExitStack

import concourse.mybir as mybir
from concourse.masks import make_identity

F32 = mybir.dt.float32
BF16 = mybir.dt.bfloat16
I32 = mybir.dt.int32
U32 = mybir.dt.uint32
U8 = mybir.dt.uint8
FP8X4 = mybir.dt.float8_e4m3fn_x4
FP4X4 = mybir.dt.float4_e2m1fn_x4
ACT = mybir.ActivationFunctionType
ALU = mybir.AluOpType

P = 128
PACK = 4
NODES = 512
FEATURES = 512
EMBED = 512
HEADS = 4
TILES = NODES // P
LAST = TILES - 1
EPS = 1e-6

FLOPS = 2 * NODES * FEATURES * EMBED + 2 * HEADS * NODES * NODES * EMBED


def tile_affnet_kernel(tc, X, W_words, W_scales, Z, beta, out):
    nc = tc.nc
    with ExitStack() as ctx:
        keep = ctx.enter_context(tc.tile_pool(name="keep", bufs=1))
        work = ctx.enter_context(tc.tile_pool(name="work", bufs=2))
        psum_t = ctx.enter_context(tc.psum_pool(name="psum_t", bufs=4))
        psum_m = ctx.enter_context(tc.psum_pool(name="psum_m", bufs=4))
        ctx.enter_context(tc.manual_schedule())

        ones = keep.tile([P, P], F32)
        nc.vector.memset(ones[:], 1.0)

        def keep_busy(times):
            idle_ps = psum_m.tile([P, P], F32, tag="m")
            for i in range(times):
                nc.tensor.matmul(out=idle_ps[:], lhsT=ones[:], rhs=ones[:], start=True, stop=True)

        keep_busy(4)

        w_plane = keep.tile([P, EMBED], U8, align_bytes=64)
        nc.vector.memset(w_plane[:].bitcast(I32), 0)
        w_plane_t = keep.tile([P, EMBED], U8, align_bytes=64)
        half = keep.tile([P, 1], F32)
        nc.vector.memset(half[:], 0.5)
        root = keep.tile([P, HEADS], F32)
        nc.vector.memset(root[:], 0.5)
        warm = keep.tile([P, 1], F32)
        nc.scalar.activation(out=warm[:], in_=half[:], func=ACT.Ln)
        ident_f = keep.tile([P, P], F32)
        make_identity(nc, ident_f[:])

        z_sb = keep.tile([P, TILES, HEADS, EMBED], BF16)
        x_sb = keep.tile([P, TILES, FEATURES], BF16)
        w_words = keep.tile([P, 2 * EMBED], U8, align_bytes=64)
        w_words_t = keep.tile([P, 2 * EMBED], U8, align_bytes=64)
        beta_b = keep.tile([P, 1], BF16)

        def load_z(j, hb):
            nc.sync.dma_start(
                out=z_sb[:, j, 2 * hb : 2 * hb + 2, :],
                in_=Z[2 * hb : 2 * hb + 2, j * P : (j + 1) * P, :].rearrange("h p e -> p h e"),
            )

        x_rows = X.rearrange("(a p) f -> p a f", p=P)
        nc.sync.dma_start(out=x_sb[:, 0:2, :], in_=x_rows[:, 0:2, :])
        nc.sync.dma_start(out=w_words[:].bitcast(I32), in_=W_words[0].bitcast(I32))
        for q in range(4):
            nc.sync.dma_start(
                out=w_plane[32 * q : 32 * q + 4, :].bitcast(I32),
                in_=W_scales[0, 4 * q : 4 * q + 4, :].bitcast(I32),
            )
        nc.sync.dma_start(out=x_sb[:, 2:4, :], in_=x_rows[:, 2:4, :])
        load_z(0, 0)
        load_z(0, 1)
        for j in range(1, TILES):
            for hb in range(2):
                load_z(j, hb)
        nc.sync.dma_start(out=beta_b[:], in_=beta.partition_broadcast(P))

        x_grouped = keep.tile([P, TILES, P, PACK], BF16, align_bytes=64)
        x_codes = keep.tile([P, NODES], U32, align_bytes=64)
        x_scales = keep.tile([P, NODES], U8, align_bytes=64)
        xe_grouped = keep.tile([P, TILES, P, PACK], BF16, align_bytes=64)
        xe_codes = keep.tile([P, NODES], U32, align_bytes=64)
        xe_scales = keep.tile([P, NODES], U8, align_bytes=64)
        x_sumsq = keep.tile([P, TILES], F32)
        x_root = keep.tile([P, TILES], F32)
        x_norm = keep.tile([P, TILES], F32)
        x_inv = keep.tile([P, TILES], F32)
        x_inv_row = keep.tile([P, NODES], F32)
        z_grouped = keep.tile([P, TILES, HEADS, P, PACK], BF16, align_bytes=64)
        z_codes = keep.tile([P, TILES, HEADS * P], U32, align_bytes=64)
        z_scales = keep.tile([P, TILES, HEADS * P], U8, align_bytes=64)
        z_sumsq = keep.tile([P, TILES, HEADS], F32)
        z_root = keep.tile([P, TILES, HEADS], F32)
        z_norm = keep.tile([P, TILES, HEADS], F32)
        z_inv = keep.tile([P, TILES, HEADS], F32)
        best = keep.tile([P, TILES, NODES], F32)
        direct = keep.tile([P, TILES, NODES], F32)
        both = keep.tile([P, LAST, NODES], F32)
        late = keep.tile([P, TILES, P], F32)
        logs = keep.tile([P, TILES, NODES], F32)
        result = keep.tile([P, TILES, NODES], F32)
        beta_f = keep.tile([P, 1], F32)

        def permute_words():
            for u in range(2):
                nc.vector.tensor_copy(
                    out=w_words_t[:, u * EMBED : (u + 1) * EMBED].rearrange("p (c q b) -> p q c b", c=2, b=2),
                    in_=w_words[:, u * EMBED : (u + 1) * EMBED].rearrange("p (q c b) -> p q c b", c=2, b=2),
                )

        def permute_scales():
            nc.vector.tensor_copy(
                out=w_plane_t[:].rearrange("p (u c q) -> p u q c", u=2, c=2),
                in_=w_plane[:].rearrange("p (u q c) -> p u q c", u=2, c=2),
            )

        def transpose_x(b):
            x_t = psum_t.tile([P, 2, 2, P], F32, tag="t")
            for a in range(2):
                for u in range(2):
                    nc.tensor.transpose(
                        x_t[:, a, u, :],
                        x_sb[:, 2 * b + a, :].bitcast(F32)[:, u : FEATURES // 2 : 2],
                        ident_f[:],
                    )
            return x_t

        def move_x(copy, b, x_t):
            copy(
                out=x_grouped[:, 2 * b : 2 * b + 2].bitcast(F32),
                in_=x_t[:].rearrange("p a u m -> p a m u"),
            )

        def quantise_x(b):
            cols = slice(2 * b * P, (2 * b + 2) * P)
            nc.vector.quantize_mx(
                out=x_codes[:, cols].bitcast(FP8X4),
                scales=x_scales[:, cols],
                in_=x_grouped[:, 2 * b : 2 * b + 2].rearrange("p a m t -> p (a m t)"),
            )

        def embed_t(a):
            xe_t = psum_m.tile([P, PACK, P], F32, tag="m")
            for t in range(PACK):
                nc.tensor.matmul_mx(
                    out=xe_t[:, t, :],
                    lhsT=w_words_t[:, 2 * P * t : 2 * P * (t + 1)].bitcast(FP4X4),
                    lhsT_scale=w_plane_t[:, P * t : P * (t + 1)],
                    rhs=x_codes[:, a * P : (a + 1) * P].bitcast(FP8X4),
                    rhs_scale=x_scales[:, a * P : (a + 1) * P],
                    start=True,
                    stop=True,
                )
            return xe_t

        def round_xe(copy, a, xe_t):
            copy(out=xe_grouped[:, a], in_=xe_t[:].rearrange("p t n -> p n t"))

        def quantise_xe():
            nc.vector.quantize_mx(
                out=xe_codes[:].bitcast(FP8X4),
                scales=xe_scales[:],
                in_=xe_grouped[:].rearrange("p a m t -> p (a m t)"),
            )

        def embed(a):
            xe_ps = psum_t.tile([P, EMBED], F32, tag="t")
            nc.tensor.matmul_mx(
                out=xe_ps[:],
                lhsT=x_codes[:, a * P : (a + 1) * P].bitcast(FP8X4),
                lhsT_scale=x_scales[:, a * P : (a + 1) * P],
                rhs=w_words[:].bitcast(FP4X4),
                rhs_scale=w_plane[:],
                start=True,
                stop=True,
            )
            return xe_ps

        def square_x(a, xe_ps):
            squares = work.tile([P, EMBED], BF16)
            nc.scalar.activation(
                out=squares[:], in_=xe_ps[:], func=ACT.Square, accum_out=x_sumsq[:, a : a + 1]
            )

        def transpose_z(j, hb):
            z_t = psum_t.tile([P, 2, 2, P], F32, tag="t")
            for h in range(2):
                for u in range(2):
                    nc.tensor.transpose(
                        z_t[:, h, u, :],
                        z_sb[:, j, 2 * hb + h, :].bitcast(F32)[:, u * P : (u + 1) * P],
                        ident_f[:],
                    )
            return z_t

        def move_z(copy, j, hb, z_t):
            copy(
                out=z_grouped[:, j, 2 * hb : 2 * hb + 2].bitcast(F32),
                in_=z_t[:].rearrange("p h u n -> p h n u"),
            )

        def square_z(j, h):
            squares = work.tile([P, EMBED], BF16)
            nc.scalar.activation(
                out=squares[:], in_=z_sb[:, j, h, :], func=ACT.Square,
                accum_out=z_sumsq[:, j, h : h + 1],
            )

        def gram(j, h, bank):
            for t in range(PACK):
                rows = z_grouped[:, j, h].rearrange("p n t -> p t n")[:, t, :]
                nc.tensor.matmul(
                    out=bank[:, h, :], lhsT=rows, rhs=rows, start=(t == 0), stop=(t == PACK - 1)
                )

        def add_diagonal(j, h, bank):
            products = work.tile([P, P], BF16)
            nc.vector.scalar_tensor_tensor(
                out=products[:], in0=bank[:, h, :], scalar=1.0, in1=ident_f[:],
                op0=ALU.mult, op1=ALU.mult, accum_out=z_sumsq[:, j, h : h + 1],
            )

        def quantise_z(j):
            nc.vector.quantize_mx(
                out=z_codes[:, j, :].bitcast(FP8X4),
                scales=z_scales[:, j, :],
                in_=z_grouped[:, j].rearrange("p h n t -> p (h n t)"),
            )

        def square_z_on_vector(j, h):
            squares = work.tile([P, EMBED], BF16)
            nc.vector.scalar_tensor_tensor(
                out=squares[:], in0=z_sb[:, j, h, :], scalar=1.0, in1=z_sb[:, j, h, :],
                op0=ALU.mult, op1=ALU.mult, accum_out=z_sumsq[:, j, h : h + 1],
            )

        def root_z(j, hb):
            pair = slice(2 * hb, 2 * hb + 2)
            nc.gpsimd.tensor_tensor(
                out=z_root[:, j, pair], in0=z_sumsq[:, j, pair], in1=root[:, :2], op=ALU.pow
            )

        def add_eps_z(j, pair):
            nc.vector.tensor_scalar_add(out=z_norm[:, j, pair], in0=z_root[:, j, pair], scalar1=EPS)

        def invert_z_norm(j, pair):
            nc.vector.reciprocal(out=z_inv[:, j, pair], in_=z_norm[:, j, pair])

        def multiply(j, heads=range(HEADS)):
            banks = []
            for h in heads:
                aff_ps = psum_m.tile([P, NODES], F32, tag="m")
                nc.tensor.matmul_mx(
                    out=aff_ps[:],
                    lhsT=z_codes[:, j, h * P : (h + 1) * P].bitcast(FP8X4),
                    lhsT_scale=z_scales[:, j, h * P : (h + 1) * P],
                    rhs=xe_codes[:].bitcast(FP8X4),
                    rhs_scale=xe_scales[:],
                    start=True,
                    stop=True,
                )
                banks.append(aff_ps)
            return banks

        def scale_head_0(j, banks):
            first = work.tile([P, NODES], F32, name="running", bufs=4)
            nc.scalar.activation(out=first[:], in_=banks[0][:], func=ACT.Copy, scale=z_inv[:, j, 0:1])
            return first

        def keep_larger(j, h, banks, running):
            if h == HEADS - 1:
                larger = best[:, j, :]
            else:
                larger = work.tile([P, NODES], F32, name="running", bufs=4)[:]
            nc.vector.scalar_tensor_tensor(
                out=larger, in0=banks[h][:], scalar=z_inv[:, j, h : h + 1], in1=running,
                op0=ALU.mult, op1=ALU.max,
            )
            return larger

        def keep_larger_half(j, h, banks, running, half_cols, larger):
            nc.vector.scalar_tensor_tensor(
                out=larger[:, half_cols], in0=banks[h][:, half_cols], scalar=z_inv[:, j, h : h + 1],
                in1=running[:, half_cols], op0=ALU.mult, op1=ALU.max,
            )

        def scale_columns(engine, j, blocks):
            cols = slice(blocks[0] * P, (blocks[-1] + 1) * P)
            engine.tensor_tensor(
                out=direct[:, j, cols], in0=best[:, j, cols], in1=x_inv_row[:, cols], op=ALU.mult
            )

        def symmetrise(j, flipped):
            width = (j + 1) * P
            nc.vector.scalar_tensor_tensor(
                out=both[:, j, :width], in0=flipped, scalar=x_inv[:, j : j + 1],
                in1=direct[:, j, :width], op0=ALU.mult, op1=ALU.add,
            )

        def log(out_ap, in_ap):
            nc.scalar.activation(out=out_ap, in_=in_ap, func=ACT.Ln, scale=0.25, bias=half[:])

        def power(out_ap, in_ap):
            nc.scalar.activation(out=out_ap, in_=in_ap, func=ACT.Exp, scale=beta_f[:])

        on_vector = nc.vector.tensor_copy
        on_scalar = nc.scalar.copy

        ALL, LOW, HIGH = slice(0, 4), slice(0, 2), slice(2, 4)
        halves = (slice(0, NODES // 2), slice(NODES // 2, NODES))

        def keep_larger_halves(j, h, banks, running):
            if h == HEADS - 1:
                larger = best[:, j, :]
            else:
                larger = work.tile([P, NODES], F32, name="running", bufs=4)[:]
            for cols in halves:
                keep_larger_half(j, h, banks, running, cols, larger)
            return larger

        x_t0 = transpose_x(0)
        permute_words()
        move_x(on_vector, 0, x_t0)
        permute_scales()
        x_t1 = transpose_x(1)
        square_z(0, 0)
        move_x(on_scalar, 1, x_t1)
        z_t0 = transpose_z(0, 0)
        z_t1 = transpose_z(0, 1)
        keep_busy(2)
        quantise_x(0)
        xe_banks = [embed_t(0), embed_t(1)]
        square_z(0, 1)
        root_z(0, 0)
        quantise_x(1)
        move_z(on_vector, 0, 0, z_t0)
        xe_banks += [embed_t(2), embed_t(3)]
        move_z(on_scalar, 0, 1, z_t1)
        round_xe(on_vector, 0, xe_banks[0])
        round_xe(on_scalar, 1, xe_banks[1])
        round_xe(on_vector, 2, xe_banks[2])
        round_xe(on_scalar, 3, xe_banks[3])
        z_t0 = transpose_z(1, 0)
        z_t1 = transpose_z(1, 1)
        square_z(0, 2)
        square_z(0, 3)
        root_z(0, 1)
        quantise_z(0)
        add_eps_z(0, LOW)
        quantise_xe()
        invert_z_norm(0, LOW)
        z_t2 = transpose_z(2, 0)
        z_t3 = transpose_z(2, 1)
        square_z(1, 0)
        square_z(1, 1)
        root_z(1, 0)
        aff = multiply(0)
        move_z(on_vector, 1, 0, z_t0)
        move_z(on_vector, 1, 1, z_t1)
        first = scale_head_0(0, aff)
        move_z(on_vector, 2, 0, z_t2)
        add_eps_z(0, HIGH)
        move_z(on_vector, 2, 1, z_t3)
        invert_z_norm(0, HIGH)
        norm_banks = [embed(0), embed(1)]
        square_z(1, 2)
        square_x(0, norm_banks[0])
        square_z(1, 3)
        root_z(1, 1)
        gram_bank = psum_t.tile([P, HEADS, P], F32, tag="t")
        gram(2, 0, gram_bank)
        gram(2, 1, gram_bank)
        norm_banks += [embed(2), embed(3)]
        gram(2, 2, gram_bank)
        gram(2, 3, gram_bank)
        square_x(1, norm_banks[1])

        running = keep_larger(0, 1, aff, first[:])
        add_eps_z(1, LOW)
        quantise_z(1)
        invert_z_norm(1, LOW)
        running = keep_larger_halves(0, 2, aff, running)
        running = keep_larger_halves(0, 3, aff, running)
        aff = multiply(1)
        square_x(2, norm_banks[2])
        square_x(3, norm_banks[3])
        nc.gpsimd.tensor_tensor(out=x_root[:], in0=x_sumsq[:], in1=root[:], op=ALU.pow)
        first = scale_head_0(1, aff)
        quantise_z(2)
        add_eps_z(1, HIGH)
        add_diagonal(2, 0, gram_bank)
        add_diagonal(2, 1, gram_bank)
        root_z(2, 0)
        add_diagonal(2, 2, gram_bank)
        add_diagonal(2, 3, gram_bank)
        root_z(2, 1)
        z_t0 = transpose_z(3, 0)
        z_t1 = transpose_z(3, 1)
        square_z(3, 0)
        move_z(on_scalar, 3, 0, z_t0)
        move_z(on_scalar, 3, 1, z_t1)
        square_z(3, 1)
        root_z(3, 0)
        invert_z_norm(1, HIGH)
        running = keep_larger_halves(1, 1, aff, first[:])
        running = keep_larger_halves(1, 2, aff, running)
        keep_larger_half(1, 3, aff, running, halves[0], best[:, 1, :])
        nc.vector.tensor_scalar_add(out=x_norm[:], in0=x_root[:], scalar1=EPS)
        add_eps_z(2, LOW)
        keep_larger_half(1, 3, aff, running, halves[1], best[:, 1, :])
        nc.vector.reciprocal(out=x_inv[:], in_=x_norm[:])
        invert_z_norm(2, LOW)
        aff = multiply(2, (0, 1, 2))
        first = scale_head_0(2, aff)
        row_ps = psum_t.tile([P, NODES], F32, tag="t")
        for a in range(TILES):
            nc.tensor.matmul(
                out=row_ps[:, a * P : (a + 1) * P],
                lhsT=x_inv[:, a : a + 1].to_broadcast([P, P]),
                rhs=ident_f[:],
                start=True,
                stop=True,
            )
        aff += multiply(2, (3,))
        quantise_z(3)
        aff3 = multiply(3, (0,))
        square_z(3, 2)
        square_z(3, 3)
        root_z(3, 1)
        nc.scalar.copy(out=x_inv_row[:], in_=row_ps[:])
        add_eps_z(2, HIGH)
        second = work.tile([P, NODES], F32, name="running", bufs=4)[:]
        keep_larger_half(2, 1, aff, first, halves[0], second)
        invert_z_norm(2, HIGH)
        keep_larger_half(2, 1, aff, first, halves[1], second)
        add_eps_z(3, LOW)
        running = keep_larger_halves(2, 2, aff, second)
        invert_z_norm(3, LOW)
        first = scale_head_0(3, aff3)[:]
        running = keep_larger_halves(2, 3, aff, running)
        aff3 += multiply(3, (1, 2))
        flip_a = psum_t.tile([P, 3, P], F32, tag="t")
        flip_b = psum_t.tile([P, 3, P], F32, tag="t")
        nc.tensor.transpose(flip_b[:, 0, :], best[:, 0, 0:P], ident_f[:])
        for i in range(2):
            nc.tensor.transpose(flip_b[:, 1 + i, :], best[:, i, P : 2 * P], ident_f[:])
        aff3 += multiply(3, (3,))
        for i in range(3):
            nc.tensor.transpose(flip_a[:, i, :], best[:, i, 2 * P : 3 * P], ident_f[:])
        scale_columns(nc.gpsimd, 2, (0, 1, 2))
        nc.gpsimd.tensor_tensor(
            out=direct[:, :LAST, LAST * P :], in0=best[:, :LAST, LAST * P :],
            in1=x_inv_row[:, LAST * P :].unsqueeze(1).broadcast_to([P, LAST, P]), op=ALU.mult,
        )
        scale_columns(nc.vector, 0, (0,))
        scale_columns(nc.vector, 1, (0, 1))
        add_eps_z(3, HIGH)
        nc.vector.tensor_copy(out=beta_f[:], in_=beta_b[:])
        running = keep_larger_halves(3, 1, aff3, first)
        invert_z_norm(3, HIGH)
        symmetrise(0, flip_b[:, 0, :])
        log(logs[:, 0, :P], both[:, 0, :P])
        running = keep_larger_halves(3, 2, aff3, running)
        symmetrise(1, flip_b[:, 1:, :].rearrange("p i n -> p (i n)"))
        log(logs[:, 1, : 2 * P], both[:, 1, : 2 * P])
        running = keep_larger_halves(3, 3, aff3, running)
        symmetrise(2, flip_a[:].rearrange("p i n -> p (i n)"))
        log(logs[:, 2, : 3 * P], both[:, 2, : 3 * P])

        late_banks = []
        for b in range(2):
            flip_c = psum_m.tile([P, 2, P], F32, tag="m")
            for i in range(2):
                nc.tensor.transpose(
                    flip_c[:, i, :], best[:, LAST, (2 * b + i) * P : (2 * b + i + 1) * P], ident_f[:]
                )
            late_banks.append(flip_c)
        scale_columns(nc.vector, LAST, (LAST,))
        for b in range(2):
            for i in range(2):
                node_tile = 2 * b + i
                nc.vector.scalar_tensor_tensor(
                    out=late[:, node_tile, :], in0=late_banks[b][:, i, :],
                    scalar=x_inv[:, node_tile : node_tile + 1], in1=direct[:, node_tile, LAST * P :],
                    op0=ALU.mult, op1=ALU.add,
                )
            log(logs[:, 2 * b : 2 * b + 2, LAST * P :], late[:, 2 * b : 2 * b + 2, :])
        mirror_a = psum_m.tile([P, 3, P], F32, tag="m")
        nc.tensor.transpose(mirror_a[:, 0, :], logs[:, 1, :P], ident_f[:])
        for i in range(2):
            nc.tensor.transpose(mirror_a[:, 1 + i, :], logs[:, 2, i * P : (i + 1) * P], ident_f[:])
        mirror_b = psum_m.tile([P, TILES, P], F32, tag="m")
        for i in range(TILES):
            nc.tensor.transpose(mirror_b[:, i, :], logs[:, i, LAST * P :], ident_f[:])
        nc.vector.tensor_copy(
            out=logs[:, 0, P : 3 * P], in_=mirror_a[:, 0:2, :].rearrange("p i n -> p (i n)")
        )
        nc.vector.tensor_copy(out=logs[:, 1, 2 * P : 3 * P], in_=mirror_a[:, 2, :])
        for j in (2, 1, 0, 3):
            if j == LAST:
                power(result[:, j, :], mirror_b[:].rearrange("p i n -> p (i n)"))
            else:
                power(result[:, j, :], logs[:, j, :])
            nc.sync.dma_start(out=out[j * P : (j + 1) * P, :], in_=result[:, j, :])
